import numpy as np
import ml_dtypes


def mxq(x, axis, fmt="e4m3"):
    dtype, down = {"e4m3": (ml_dtypes.float8_e4m3fn, 7), "e5m2": (ml_dtypes.float8_e5m2, 14)}[fmt]
    v = np.moveaxis(np.asarray(x, np.float32).astype(ml_dtypes.bfloat16).astype(np.float64), axis, -1)
    blocks = v.reshape(v.shape[:-1] + (-1, 32))
    amax = np.abs(blocks).max(-1, keepdims=True)
    byte = np.maximum(np.where(amax > 0, np.frexp(amax)[1] - 1 + 127, 0) - down, 1)
    scale = np.exp2(byte - 127.0)
    codes = (blocks / scale).astype(np.float32).astype(dtype).astype(np.float64)
    return np.moveaxis((codes * scale).reshape(v.shape), -1, axis)


WIDE = False


def mx_kscale(k):
    if not WIDE:
        return np.ones(k)
    levels = np.array([10, -10, 5, -5, 0])
    if k % 512:
        return np.exp2(np.random.permutation(np.resize(levels, k // 32))).repeat(32)
    a = np.empty((k // 512, 16))
    for p in range(k // 512):
        a[p, :8] = np.random.permutation(np.resize(levels, 8))
        for g in range(8):
            far = levels[np.abs(levels - a[p, g]) >= 10]
            a[p, g + 8] = far[np.random.randint(len(far))]
    return np.exp2(a.ravel()).repeat(32)


BF16 = ml_dtypes.bfloat16


def bf(x):
    return np.asarray(x, np.float32).astype(BF16)


def f64(x):
    return np.asarray(x).astype(np.float64)


N, F, K, D, E = 512, 2048, 1536, 1024, 1024
QS = 2.0
PS = 16.0


def setup_inputs():
    s, t = mx_kscale(F), mx_kscale(E)
    return {"x": bf(np.random.standard_normal((N, F)) * s),
            "Wy_w": bf(np.random.standard_normal((E, F)) * QS * F ** -0.5 / s[None, :] * t[:, None]),
            "Wy_b": bf(np.random.standard_normal(E) * 0.2 * t),
            "k": bf(np.random.standard_normal((K, E)) / t[None, :]),
            "prior": bf(np.random.uniform(size=K) * PS)}


def reference(x, Wy_w, Wy_b, k, prior):
    scale = 1.0 / (E ** 0.5)
    q = (mxq(f64(x), 1, "e4m3") @ mxq(f64(Wy_w), 1, "e4m3").T) + f64(Wy_b)
    sc = (mxq(q, 1, "e4m3") @ mxq(f64(k), 1, "e4m3").T) * scale
    e = np.exp(sc - sc.max(-1, keepdims=True))
    att = e / e.sum(-1, keepdims=True)
    return att * f64(prior)[None, :]

@@ -1,0 +1,292 @@
+from contextlib import ExitStack
+
+import concourse.masks as masks
+import concourse.mybir as mybir
+
+F32 = mybir.dt.float32
+BF16 = mybir.dt.bfloat16
+U32 = mybir.dt.uint32
+U8 = mybir.dt.uint8
+FP8X4 = mybir.dt.float8_e4m3fn_x4
+ALU = mybir.AluOpType
+ACT = mybir.ActivationFunctionType
+AXIS = mybir.AxisListType
+
+P = 128
+BANK = 512
+N_ROWS, F_DIM, E_DIM, K_DICT = 512, 2048, 1024, 1536
+N_BLOCKS = N_ROWS // P
+F_PASSES = F_DIM // 512
+E_PASSES = E_DIM // 512
+J_CHUNKS = K_DICT // BANK
+UNIT = 4096
+SCALE = 1.0 / (E_DIM**0.5)
+
+FLOPS = 2 * N_ROWS * F_DIM * E_DIM + 2 * N_ROWS * E_DIM * K_DICT
+
+
+def tile_visualdeconfounder_pa_kernel(tc, x, Wy_w, Wy_b, k, prior, out):
+    nc = tc.nc
+    with ExitStack() as ctx:
+        ctx.enter_context(tc.manual_schedule())
+        const = ctx.enter_context(tc.tile_pool(name="const", bufs=1))
+        raw_pool = ctx.enter_context(tc.tile_pool(name="raw", bufs=1))
+        keep = ctx.enter_context(tc.tile_pool(name="keep", bufs=1))
+        grouped_pool = ctx.enter_context(tc.tile_pool(name="grouped", bufs=3))
+        soft = ctx.enter_context(tc.tile_pool(name="soft", bufs=3))
+        small = ctx.enter_context(tc.tile_pool(name="small", bufs=2))
+
+        x_raw = [raw_pool.tile([P, UNIT], BF16, name="x_raw%d" % a) for a in range(2)]
+        w_raw = [raw_pool.tile([P, UNIT], BF16, name="w_raw%d" % c) for c in range(4)]
+        k_raw = [raw_pool.tile([P, UNIT], BF16, name="k_raw%d" % c) for c in range(J_CHUNKS)]
+        def load_w(c):
+            g, h = divmod(c, 2)
+            rows = Wy_w[512 * g : 512 * (g + 1), :].rearrange("(p t) f -> p t f", t=4)
+            nc.sync.dma_start(
+                out=w_raw[c][:].rearrange("p (s f) -> p s f", s=2), in_=rows[:, 2 * h : 2 * h + 2, :]
+            )
+
+        def load_k(c):
+            rows = k[BANK * c : BANK * (c + 1), :]
+            nc.sync.dma_start(
+                out=k_raw[c][:].rearrange("p (b e) -> p b e", b=4),
+                in_=rows.rearrange("(b p) e -> p b e", p=P),
+            )
+
+        def load_x(a):
+            for b in range(2):
+                i = 2 * a + b
+                nc.sync.dma_start(
+                    out=x_raw[a][:, F_DIM * b : F_DIM * (b + 1)], in_=x[P * i : P * (i + 1), :]
+                )
+
+        load_x(0)
+        load_w(0)
+        load_w(1)
+        bias_bf = const.tile([P, 8], BF16)
+        with nc.allow_non_contiguous_dma(reason="1,024 bias values, four to a piece"):
+            nc.sync.dma_start(
+                out=bias_bf[:].rearrange("p (g t) -> p g t", t=4),
+                in_=Wy_b.rearrange("(g p t) -> p g t", p=P, t=4),
+            )
+        load_w(2)
+        load_w(3)
+        load_k(0)
+        load_k(1)
+        load_k(2)
+        load_x(1)
+        prior_all = const.tile([P, K_DICT], BF16)
+        nc.sync.dma_start(out=prior_all[:], in_=prior.partition_broadcast(P))
+
+        zero = const.tile([P, 1], F32)
+        one = const.tile([P, 1], F32)
+        nc.vector.memset(zero[:], 0.0)
+        nc.scalar.activation(out=one[:], in_=zero[:], func=ACT.Exp)
+
+        ident = const.tile([P, P], F32)
+        masks.make_identity(nc, ident[:])
+
+        bias = const.tile([P, 8], F32)
+
+        x_codes = keep.tile([P, N_BLOCKS * F_PASSES * P], U32, align_bytes=64)
+        x_scales = keep.tile([P, N_BLOCKS * F_PASSES * P], U8, align_bytes=64)
+        w_codes = keep.tile([P, 8 * F_PASSES * P], U32, align_bytes=64)
+        w_scales = keep.tile([P, 8 * F_PASSES * P], U8, align_bytes=64)
+        k_codes = keep.tile([P, E_PASSES * K_DICT], U32, align_bytes=64)
+        k_scales = keep.tile([P, E_PASSES * K_DICT], U8, align_bytes=64)
+        q_codes = keep.tile([P, E_PASSES * N_ROWS], U32, align_bytes=64)
+        q_scales = keep.tile([P, E_PASSES * N_ROWS], U8, align_bytes=64)
+        q_grouped = [
+            keep.tile([P, N_ROWS * 4], BF16, name="q_grouped%d" % g, align_bytes=64)
+            for g in range(E_PASSES)
+        ]
+
+        def quantise(grouped, codes, scales, first, width):
+            nc.vector.quantize_mx(
+                out=codes[:, first : first + width].bitcast(FP8X4),
+                scales=scales[:, first : first + width],
+                in_=grouped,
+            )
+
+        def mx_pass(acc, a_codes, a_scales, a_first, b_codes, b_scales, b_first, width, g, passes):
+            nc.tensor.matmul_mx(
+                out=acc,
+                lhsT=a_codes[:, a_first : a_first + P].bitcast(FP8X4),
+                lhsT_scale=a_scales[:, a_first : a_first + P],
+                rhs=b_codes[:, b_first : b_first + width].bitcast(FP8X4),
+                rhs_scale=b_scales[:, b_first : b_first + width],
+                start=(g == 0),
+                stop=(g == passes - 1),
+            )
+
+        q_psum = ctx.enter_context(tc.psum_pool(name="q_psum", bufs=2))
+
+        def new_q_banks():
+            return [q_psum.tile([P, 4, P], F32, name="q_bank%d" % b, tag="q_bank") for b in range(2)]
+
+        def first_product(c, s, a, q_banks):
+            t = 2 * (c % 2) + s
+            for b in range(2):
+                for g in range(F_PASSES):
+                    mx_pass(
+                        q_banks[b][:, t, :],
+                        w_codes, w_scales, ((2 * c + s) * F_PASSES + g) * P,
+                        x_codes, x_scales, ((2 * a + b) * F_PASSES + g) * P,
+                        P, g, F_PASSES,
+                    )
+
+        def finish_q(g, a, q_banks):
+            bias_tn = bias[:, 4 * g : 4 * g + 4].unsqueeze(1).to_broadcast([P, P, 4])
+            for b in range(2):
+                i = 2 * a + b
+                nc.vector.tensor_tensor(
+                    out=q_grouped[g][:, BANK * i : BANK * (i + 1)].rearrange("p (n t) -> p n t", t=4),
+                    in0=q_banks[b][:].rearrange("p t n -> p n t"),
+                    in1=bias_tn,
+                    op=ALU.add,
+                )
+            for b in range(2):
+                i = 2 * a + b
+                quantise(
+                    q_grouped[g][:, BANK * i : BANK * (i + 1)], q_codes, q_scales, g * N_ROWS + P * i, P
+                )
+
+        x_units = [
+            (x_raw[a], False, x_codes, x_scales, [2 * a * BANK, (2 * a + 1) * BANK]) for a in range(2)
+        ]
+        w_units = [
+            (w_raw[c], False, w_codes, w_scales, [2 * c * BANK, (2 * c + 1) * BANK]) for c in range(4)
+        ]
+        k_units = [
+            (k_raw[c], True, k_codes, k_scales, [BANK * c, K_DICT + BANK * c]) for c in range(J_CHUNKS)
+        ]
+
+        def quantise_unit(unit, grouped):
+            for h in range(2):
+                quantise(grouped[:, 2048 * h : 2048 * (h + 1)], unit[2], unit[3], unit[4][h], BANK)
+
+        with tc.psum_pool(name="t_psum", bufs=6) as t_psum:
+
+            def transpose_unit(unit):
+                words = unit[0][:].bitcast(F32)
+                grouped = grouped_pool.tile([P, UNIT], BF16, align_bytes=64)
+                order = "p (g b r u) -> p b g r u" if unit[1] else "p (b g r u) -> p b g r u"
+                dest = grouped[:].bitcast(F32).rearrange(order, g=2, b=4, u=2)
+                for b in range(4):
+                    bank = t_psum.tile([P, 4, P], F32)
+                    for v in range(4):
+                        g, u = divmod(v, 2)
+                        first = BANK * b + 2 * P * g
+                        nc.tensor.transpose(
+                            bank[:, v, :], words[:, first + u : first + 2 * P : 2], ident[:]
+                        )
+                    nc.scalar.copy(
+                        out=dest[:, b], in_=bank[:].rearrange("p (g u) r -> p g r u", u=2)
+                    )
+                return grouped
+
+            for unit in [x_units[0], w_units[0]]:
+                quantise_unit(unit, transpose_unit(unit))
+            later_units = w_units[1:] + k_units
+            q_banks = []
+            for group in range(8):
+                c, s = divmod(group, 2)
+                grouped = transpose_unit(later_units[group]) if group < len(later_units) else None
+                if group % 4 == 0:
+                    q_banks = new_q_banks()
+                first_product(c, s, 0, q_banks)
+                if group == 0:
+                    nc.vector.tensor_copy(out=bias[:], in_=bias_bf[:])
+                if group % 4 == 3:
+                    finish_q(group // 4, 0, q_banks)
+                if group < len(later_units):
+                    quantise_unit(later_units[group], grouped)
+            quantise_unit(x_units[1], transpose_unit(x_units[1]))
+
+        with tc.psum_pool(name="s_psum", bufs=6, reuse_waits="tile") as s_psum:
+
+            def scores(i):
+                banks = []
+                for c in range(J_CHUNKS):
+                    bank = s_psum.tile([P, BANK], F32, name="s_bank")
+                    for g in range(E_PASSES):
+                        mx_pass(
+                            bank[:],
+                            q_codes, q_scales, g * N_ROWS + P * i,
+                            k_codes, k_scales, g * K_DICT + BANK * c,
+                            BANK, g, E_PASSES,
+                        )
+                    banks.append(bank)
+                return banks
+
+            def row_maximum(banks):
+                chunk_max = small.tile([P, J_CHUNKS], F32)
+                for c in range(J_CHUNKS):
+                    nc.vector.tensor_reduce(
+                        out=chunk_max[:, c : c + 1], in_=banks[c][:], axis=AXIS.X, op=ALU.max
+                    )
+                row_max = small.tile([P, 1], F32)
+                nc.vector.tensor_reduce(out=row_max[:], in_=chunk_max[:], axis=AXIS.X, op=ALU.max)
+                shift = small.tile([P, 1], F32)
+                nc.vector.tensor_scalar_mul(shift[:], row_max[:], -SCALE)
+                return shift
+
+            def maximum_of(i):
+                banks = scores(i)
+                return banks, row_maximum(banks)
+
+            def exponentials(banks, shift):
+                e = soft.tile([P, K_DICT], F32)
+                result = soft.tile([P, K_DICT], F32)
+                chunk_sum = small.tile([P, J_CHUNKS], F32)
+                for c in range(J_CHUNKS):
+                    cols = slice(BANK * c, BANK * (c + 1))
+                    nc.scalar.activation(
+                        out=e[:, cols],
+                        in_=banks[c][:],
+                        func=ACT.Exp,
+                        bias=shift[:],
+                        scale=SCALE,
+                        accum_out=chunk_sum[:, c : c + 1],
+                    )
+                    if c < J_CHUNKS - 1:
+                        nc.gpsimd.tensor_tensor(
+                            out=result[:, cols], in0=e[:, cols], in1=prior_all[:, cols], op=ALU.mult
+                        )
+                return e, result, chunk_sum
+
+            def normalise_and_store(i, e, result, chunk_sum):
+                rows = out[P * i : P * (i + 1), :]
+                first, last = slice(0, K_DICT - BANK), slice(K_DICT - BANK, K_DICT)
+                row_sum = small.tile([P, 1], F32)
+                nc.vector.tensor_reduce(out=row_sum[:], in_=chunk_sum[:], axis=AXIS.X, op=ALU.add)
+                inverse = small.tile([P, 1], F32)
+                nc.vector.reciprocal(inverse[:], row_sum[:])
+                nc.vector.scalar_tensor_tensor(
+                    out=result[:, last],
+                    in0=e[:, last],
+                    scalar=inverse[:],
+                    in1=prior_all[:, last],
+                    op0=ALU.mult,
+                    op1=ALU.mult,
+                )
+                nc.sync.dma_start(out=rows[:, last], in_=result[:, last])
+                nc.scalar.activation(
+                    out=result[:, first], in_=result[:, first], func=ACT.Copy, scale=inverse[:]
+                )
+                nc.sync.dma_start(out=rows[:, first], in_=result[:, first])
+
+            started = [exponentials(*maximum_of(i)) for i in range(2)]
+            q_banks = new_q_banks()
+            for t in range(4):
+                first_product(t // 2, t % 2, 1, q_banks)
+            finish_q(0, 1, q_banks)
+            normalise_and_store(0, *started[0])
+            q_banks = new_q_banks()
+            for t in range(4):
+                first_product(2 + t // 2, t % 2, 1, q_banks)
+            normalise_and_store(1, *started[1])
+            finish_q(1, 1, q_banks)
+            started = [exponentials(*maximum_of(i)) for i in range(2, 4)]
+            normalise_and_store(2, *started[0])
+            normalise_and_store(3, *started[1])

@@ -32,13 +32,16 @@ def tile_visualdeconfounder_pa_kernel(tc, x, Wy_w, Wy_b, k, prior, out):
         const = ctx.enter_context(tc.tile_pool(name="const", bufs=1))
         raw_pool = ctx.enter_context(tc.tile_pool(name="raw", bufs=1))
         keep = ctx.enter_context(tc.tile_pool(name="keep", bufs=1))
+        split_pool = ctx.enter_context(tc.tile_pool(name="split", bufs=2))
         grouped_pool = ctx.enter_context(tc.tile_pool(name="grouped", bufs=3))
         soft = ctx.enter_context(tc.tile_pool(name="soft", bufs=3))
         small = ctx.enter_context(tc.tile_pool(name="small", bufs=2))
+        psum = ctx.enter_context(tc.psum_pool(name="psum", bufs=6))
 
         x_raw = [raw_pool.tile([P, UNIT], BF16, name="x_raw%d" % a) for a in range(2)]
         w_raw = [raw_pool.tile([P, UNIT], BF16, name="w_raw%d" % c) for c in range(4)]
         k_raw = [raw_pool.tile([P, UNIT], BF16, name="k_raw%d" % c) for c in range(J_CHUNKS)]
+
         def load_w(c):
             g, h = divmod(c, 2)
             rows = Wy_w[512 * g : 512 * (g + 1), :].rearrange("(p t) f -> p t f", t=4)
@@ -71,10 +74,10 @@ def tile_visualdeconfounder_pa_kernel(tc, x, Wy_w, Wy_b, k, prior, out):
             )
         load_w(2)
         load_w(3)
+        load_x(1)
         load_k(0)
         load_k(1)
         load_k(2)
-        load_x(1)
         prior_all = const.tile([P, K_DICT], BF16)
         nc.sync.dma_start(out=prior_all[:], in_=prior.partition_broadcast(P))
 
@@ -119,174 +122,192 @@ def tile_visualdeconfounder_pa_kernel(tc, x, Wy_w, Wy_b, k, prior, out):
                 stop=(g == passes - 1),
             )
 
-        q_psum = ctx.enter_context(tc.psum_pool(name="q_psum", bufs=2))
+        q_banks = {}
 
-        def new_q_banks():
-            return [q_psum.tile([P, 4, P], F32, name="q_bank%d" % b, tag="q_bank") for b in range(2)]
-
-        def first_product(c, s, a, q_banks):
-            t = 2 * (c % 2) + s
+        def first_product(c, a):
+            g, h = divmod(c, 2)
+            if h == 0:
+                q_banks[g, a] = [
+                    psum.tile([P, 4, P], F32, name="q_bank%d" % b, tag="q", bufs=2) for b in range(2)
+                ]
             for b in range(2):
-                for g in range(F_PASSES):
-                    mx_pass(
-                        q_banks[b][:, t, :],
-                        w_codes, w_scales, ((2 * c + s) * F_PASSES + g) * P,
-                        x_codes, x_scales, ((2 * a + b) * F_PASSES + g) * P,
-                        P, g, F_PASSES,
-                    )
+                for s in range(2):
+                    for f in range(F_PASSES):
+                        mx_pass(
+                            q_banks[g, a][b][:, 2 * h + s, :],
+                            w_codes, w_scales, ((2 * c + s) * F_PASSES + f) * P,
+                            x_codes, x_scales, ((2 * a + b) * F_PASSES + f) * P,
+                            P, f, F_PASSES,
+                        )
 
-        def finish_q(g, a, q_banks):
+        def add_bias(g, a):
             bias_tn = bias[:, 4 * g : 4 * g + 4].unsqueeze(1).to_broadcast([P, P, 4])
             for b in range(2):
                 i = 2 * a + b
                 nc.vector.tensor_tensor(
                     out=q_grouped[g][:, BANK * i : BANK * (i + 1)].rearrange("p (n t) -> p n t", t=4),
-                    in0=q_banks[b][:].rearrange("p t n -> p n t"),
+                    in0=q_banks[g, a][b][:].rearrange("p t n -> p n t"),
                     in1=bias_tn,
                     op=ALU.add,
                 )
-            for b in range(2):
-                i = 2 * a + b
-                quantise(
-                    q_grouped[g][:, BANK * i : BANK * (i + 1)], q_codes, q_scales, g * N_ROWS + P * i, P
-                )
+
+        def quantise_q(g, a):
+            first = BANK * 2 * a
+            quantise(
+                q_grouped[g][:, first : first + 2 * BANK], q_codes, q_scales, g * N_ROWS + 2 * P * a, 2 * P
+            )
 
         x_units = [
-            (x_raw[a], False, x_codes, x_scales, [2 * a * BANK, (2 * a + 1) * BANK]) for a in range(2)
+            (x_raw[a], False, a > 0, x_codes, x_scales, [2 * a * BANK, (2 * a + 1) * BANK])
+            for a in range(2)
         ]
         w_units = [
-            (w_raw[c], False, w_codes, w_scales, [2 * c * BANK, (2 * c + 1) * BANK]) for c in range(4)
+            (w_raw[c], False, c > 0, w_codes, w_scales, [2 * c * BANK, (2 * c + 1) * BANK])
+            for c in range(4)
         ]
         k_units = [
-            (k_raw[c], True, k_codes, k_scales, [BANK * c, K_DICT + BANK * c]) for c in range(J_CHUNKS)
+            (k_raw[c], True, True, k_codes, k_scales, [BANK * c, K_DICT + BANK * c])
+            for c in range(J_CHUNKS)
         ]
 
-        def quantise_unit(unit, grouped):
+        def split_half(unit, words, h):
+            cols = slice(1024 * h, 1024 * (h + 1))
+            nc.vector.tensor_copy(
+                out=words[:, cols].rearrange("p (g u m) -> p g u m", u=2, m=P),
+                in_=unit[0][:].bitcast(F32)[:, cols].rearrange("p (g m u) -> p g u m", u=2, m=P),
+            )
+
+        def transpose_unit(unit, words):
+            grouped = grouped_pool.tile([P, UNIT], BF16, align_bytes=64)
+            order = "p (g b r u) -> p b g r u" if unit[1] else "p (b g r u) -> p b g r u"
+            dest = grouped[:].bitcast(F32).rearrange(order, g=2, b=4, u=2)
+            for b in range(4):
+                bank = psum.tile([P, 4, P], F32, name="t_bank", tag="work")
+                for v in range(4):
+                    g, u = divmod(v, 2)
+                    first = BANK * b + 2 * P * g
+                    if unit[2]:
+                        plane = words[:, first + P * u : first + P * (u + 1)]
+                    else:
+                        plane = words[:, first + u : first + 2 * P : 2]
+                    nc.tensor.transpose(bank[:, v, :], plane, ident[:])
+                nc.scalar.copy(out=dest[:, b], in_=bank[:].rearrange("p (g u) r -> p g r u", u=2))
+            return grouped
+
+        def quantise_half(unit, grouped, h):
+            quantise(grouped[:, 2048 * h : 2048 * (h + 1)], unit[3], unit[4], unit[5][h], BANK)
+
+        steps = [
+            (x_units[0], None),
+            (w_units[0], None),
+            (w_units[1], (0, 0)),
+            (w_units[2], (1, 0)),
+            (w_units[3], (2, 0)),
+            (x_units[1], (3, 0)),
+            (k_units[0], (0, 1)),
+            (k_units[1], (1, 1)),
+            (k_units[2], (2, 1)),
+        ]
+        words = steps[0][0][0][:].bitcast(F32)
+        for j, (unit, product) in enumerate(steps):
+            grouped = transpose_unit(unit, words)
+            if product:
+                first_product(*product)
+            following = steps[j + 1][0] if j + 1 < len(steps) else None
+            if following and following[2]:
+                split = split_pool.tile([P, UNIT // 2], F32, name="split")
+                words = split[:]
+            elif following:
+                words = following[0][:].bitcast(F32)
             for h in range(2):
-                quantise(grouped[:, 2048 * h : 2048 * (h + 1)], unit[2], unit[3], unit[4][h], BANK)
+                if following and following[2]:
+                    split_half(following, words, h)
+                quantise_half(unit, grouped, h)
+            if j == 2:
+                nc.vector.tensor_copy(out=bias[:], in_=bias_bf[:])
+            if product and product[0] % 2 == 1:
+                add_bias(product[0] // 2, product[1])
+            if j > 0 and steps[j - 1][1] and steps[j - 1][1][0] % 2 == 1:
+                quantise_q(steps[j - 1][1][0] // 2, steps[j - 1][1][1])
+        first_product(3, 1)
+        add_bias(1, 1)
+        quantise_q(1, 1)
 
-        with tc.psum_pool(name="t_psum", bufs=6) as t_psum:
-
-            def transpose_unit(unit):
-                words = unit[0][:].bitcast(F32)
-                grouped = grouped_pool.tile([P, UNIT], BF16, align_bytes=64)
-                order = "p (g b r u) -> p b g r u" if unit[1] else "p (b g r u) -> p b g r u"
-                dest = grouped[:].bitcast(F32).rearrange(order, g=2, b=4, u=2)
-                for b in range(4):
-                    bank = t_psum.tile([P, 4, P], F32)
-                    for v in range(4):
-                        g, u = divmod(v, 2)
-                        first = BANK * b + 2 * P * g
-                        nc.tensor.transpose(
-                            bank[:, v, :], words[:, first + u : first + 2 * P : 2], ident[:]
-                        )
-                    nc.scalar.copy(
-                        out=dest[:, b], in_=bank[:].rearrange("p (g u) r -> p g r u", u=2)
-                    )
-                return grouped
-
-            for unit in [x_units[0], w_units[0]]:
-                quantise_unit(unit, transpose_unit(unit))
-            later_units = w_units[1:] + k_units
-            q_banks = []
-            for group in range(8):
-                c, s = divmod(group, 2)
-                grouped = transpose_unit(later_units[group]) if group < len(later_units) else None
-                if group % 4 == 0:
-                    q_banks = new_q_banks()
-                first_product(c, s, 0, q_banks)
-                if group == 0:
-                    nc.vector.tensor_copy(out=bias[:], in_=bias_bf[:])
-                if group % 4 == 3:
-                    finish_q(group // 4, 0, q_banks)
-                if group < len(later_units):
-                    quantise_unit(later_units[group], grouped)
-            quantise_unit(x_units[1], transpose_unit(x_units[1]))
-
-        with tc.psum_pool(name="s_psum", bufs=6, reuse_waits="tile") as s_psum:
-
-            def scores(i):
-                banks = []
-                for c in range(J_CHUNKS):
-                    bank = s_psum.tile([P, BANK], F32, name="s_bank")
-                    for g in range(E_PASSES):
-                        mx_pass(
-                            bank[:],
-                            q_codes, q_scales, g * N_ROWS + P * i,
-                            k_codes, k_scales, g * K_DICT + BANK * c,
-                            BANK, g, E_PASSES,
-                        )
-                    banks.append(bank)
-                return banks
-
-            def row_maximum(banks):
-                chunk_max = small.tile([P, J_CHUNKS], F32)
-                for c in range(J_CHUNKS):
-                    nc.vector.tensor_reduce(
-                        out=chunk_max[:, c : c + 1], in_=banks[c][:], axis=AXIS.X, op=ALU.max
-                    )
-                row_max = small.tile([P, 1], F32)
-                nc.vector.tensor_reduce(out=row_max[:], in_=chunk_max[:], axis=AXIS.X, op=ALU.max)
-                shift = small.tile([P, 1], F32)
-                nc.vector.tensor_scalar_mul(shift[:], row_max[:], -SCALE)
-                return shift
-
-            def maximum_of(i):
-                banks = scores(i)
-                return banks, row_maximum(banks)
-
-            def exponentials(banks, shift):
-                e = soft.tile([P, K_DICT], F32)
-                result = soft.tile([P, K_DICT], F32)
-                chunk_sum = small.tile([P, J_CHUNKS], F32)
-                for c in range(J_CHUNKS):
-                    cols = slice(BANK * c, BANK * (c + 1))
-                    nc.scalar.activation(
-                        out=e[:, cols],
-                        in_=banks[c][:],
-                        func=ACT.Exp,
-                        bias=shift[:],
-                        scale=SCALE,
-                        accum_out=chunk_sum[:, c : c + 1],
-                    )
-                    if c < J_CHUNKS - 1:
-                        nc.gpsimd.tensor_tensor(
-                            out=result[:, cols], in0=e[:, cols], in1=prior_all[:, cols], op=ALU.mult
-                        )
-                return e, result, chunk_sum
-
-            def normalise_and_store(i, e, result, chunk_sum):
-                rows = out[P * i : P * (i + 1), :]
-                first, last = slice(0, K_DICT - BANK), slice(K_DICT - BANK, K_DICT)
-                row_sum = small.tile([P, 1], F32)
-                nc.vector.tensor_reduce(out=row_sum[:], in_=chunk_sum[:], axis=AXIS.X, op=ALU.add)
-                inverse = small.tile([P, 1], F32)
-                nc.vector.reciprocal(inverse[:], row_sum[:])
-                nc.vector.scalar_tensor_tensor(
-                    out=result[:, last],
-                    in0=e[:, last],
-                    scalar=inverse[:],
-                    in1=prior_all[:, last],
-                    op0=ALU.mult,
-                    op1=ALU.mult,
+        def scores(i):
+            banks = []
+            for c in range(J_CHUNKS):
+                in_q = (J_CHUNKS * i + c) % 8 >= 6
+                bank = psum.tile(
+                    [P, BANK], F32, name="s_bank", tag="q" if in_q else "work", bufs=2 if in_q else 6
                 )
-                nc.sync.dma_start(out=rows[:, last], in_=result[:, last])
+                for g in range(E_PASSES):
+                    mx_pass(
+                        bank[:],
+                        q_codes, q_scales, g * N_ROWS + P * i,
+                        k_codes, k_scales, g * K_DICT + BANK * c,
+                        BANK, g, E_PASSES,
+                    )
+                banks.append(bank)
+            return banks
+
+        def row_maximum(banks):
+            chunk_max = small.tile([P, J_CHUNKS], F32)
+            for c in range(J_CHUNKS):
+                nc.vector.tensor_reduce(
+                    out=chunk_max[:, c : c + 1], in_=banks[c][:], axis=AXIS.X, op=ALU.max
+                )
+            row_max = small.tile([P, 1], F32)
+            nc.vector.tensor_reduce(out=row_max[:], in_=chunk_max[:], axis=AXIS.X, op=ALU.max)
+            shift = small.tile([P, 1], F32)
+            nc.vector.tensor_scalar_mul(shift[:], row_max[:], -SCALE)
+            return shift
+
+        def exponentials(banks, shift):
+            e = soft.tile([P, K_DICT], F32)
+            result = soft.tile([P, K_DICT], F32)
+            chunk_sum = small.tile([P, J_CHUNKS], F32)
+            for c in range(J_CHUNKS):
+                cols = slice(BANK * c, BANK * (c + 1))
                 nc.scalar.activation(
-                    out=result[:, first], in_=result[:, first], func=ACT.Copy, scale=inverse[:]
+                    out=e[:, cols],
+                    in_=banks[c][:],
+                    func=ACT.Exp,
+                    bias=shift[:],
+                    scale=SCALE,
+                    accum_out=chunk_sum[:, c : c + 1],
                 )
-                nc.sync.dma_start(out=rows[:, first], in_=result[:, first])
+                if c < J_CHUNKS - 1:
+                    nc.gpsimd.tensor_tensor(
+                        out=result[:, cols], in0=e[:, cols], in1=prior_all[:, cols], op=ALU.mult
+                    )
+            return e, result, chunk_sum
 
-            started = [exponentials(*maximum_of(i)) for i in range(2)]
-            q_banks = new_q_banks()
-            for t in range(4):
-                first_product(t // 2, t % 2, 1, q_banks)
-            finish_q(0, 1, q_banks)
-            normalise_and_store(0, *started[0])
-            q_banks = new_q_banks()
-            for t in range(4):
-                first_product(2 + t // 2, t % 2, 1, q_banks)
-            normalise_and_store(1, *started[1])
-            finish_q(1, 1, q_banks)
-            started = [exponentials(*maximum_of(i)) for i in range(2, 4)]
-            normalise_and_store(2, *started[0])
-            normalise_and_store(3, *started[1])
+        def normalise_and_store(i, e, result, chunk_sum):
+            rows = out[P * i : P * (i + 1), :]
+            first, last = slice(0, K_DICT - BANK), slice(K_DICT - BANK, K_DICT)
+            row_sum = small.tile([P, 1], F32)
+            nc.vector.tensor_reduce(out=row_sum[:], in_=chunk_sum[:], axis=AXIS.X, op=ALU.add)
+            inverse = small.tile([P, 1], F32)
+            nc.vector.reciprocal(inverse[:], row_sum[:])
+            nc.vector.scalar_tensor_tensor(
+                out=result[:, last],
+                in0=e[:, last],
+                scalar=inverse[:],
+                in1=prior_all[:, last],
+                op0=ALU.mult,
+                op1=ALU.mult,
+            )
+            nc.sync.dma_start(out=rows[:, last], in_=result[:, last])
+            nc.scalar.activation(
+                out=result[:, first], in_=result[:, first], func=ACT.Copy, scale=inverse[:]
+            )
+            nc.sync.dma_start(out=rows[:, first], in_=result[:, first])
+
+        pending = None
+        for i in range(N_BLOCKS):
+            banks = scores(i)
+            started = exponentials(banks, row_maximum(banks))
+            if pending:
+                normalise_and_store(i - 1, *pending)
+            pending = started
+        normalise_and_store(N_BLOCKS - 1, *pending)

@@ -28,17 +28,19 @@ FLOPS = 2 * N_ROWS * F_DIM * E_DIM + 2 * N_ROWS * E_DIM * K_DICT
 def tile_visualdeconfounder_pa_kernel(tc, x, Wy_w, Wy_b, k, prior, out):
     nc = tc.nc
     with ExitStack() as ctx:
-        ctx.enter_context(tc.manual_schedule())
         const = ctx.enter_context(tc.tile_pool(name="const", bufs=1))
         raw_pool = ctx.enter_context(tc.tile_pool(name="raw", bufs=1))
         keep = ctx.enter_context(tc.tile_pool(name="keep", bufs=1))
         split_pool = ctx.enter_context(tc.tile_pool(name="split", bufs=2))
         grouped_pool = ctx.enter_context(tc.tile_pool(name="grouped", bufs=3))
-        soft = ctx.enter_context(tc.tile_pool(name="soft", bufs=3))
-        small = ctx.enter_context(tc.tile_pool(name="small", bufs=2))
-        psum = ctx.enter_context(tc.psum_pool(name="psum", bufs=6))
+        soft = ctx.enter_context(tc.tile_pool(name="soft", bufs=1))
+        small = ctx.enter_context(tc.tile_pool(name="small", bufs=4))
+        psum = ctx.enter_context(tc.psum_pool(name="psum", bufs=1))
 
-        x_raw = [raw_pool.tile([P, UNIT], BF16, name="x_raw%d" % a) for a in range(2)]
+        def new_bank(b):
+            return psum.tile([P, 4, P], F32, name="bank%d" % b)
+
+        x_raw = [raw_pool.tile([P, F_DIM], BF16, name="x_raw%d" % i) for i in range(N_BLOCKS)]
         w_raw = [raw_pool.tile([P, UNIT], BF16, name="w_raw%d" % c) for c in range(4)]
         k_raw = [raw_pool.tile([P, UNIT], BF16, name="k_raw%d" % c) for c in range(J_CHUNKS)]
 
@@ -56,28 +58,26 @@ def tile_visualdeconfounder_pa_kernel(tc, x, Wy_w, Wy_b, k, prior, out):
                 in_=rows.rearrange("(b p) e -> p b e", p=P),
             )
 
-        def load_x(a):
-            for b in range(2):
-                i = 2 * a + b
-                nc.sync.dma_start(
-                    out=x_raw[a][:, F_DIM * b : F_DIM * (b + 1)], in_=x[P * i : P * (i + 1), :]
-                )
+        def load_x(i):
+            nc.sync.dma_start(out=x_raw[i][:], in_=x[P * i : P * (i + 1), :])
 
         load_x(0)
+        load_x(1)
         load_w(0)
         load_w(1)
-        bias_bf = const.tile([P, 8], BF16)
+        bias = const.tile([P, 8], BF16)
         with nc.allow_non_contiguous_dma(reason="1,024 bias values, four to a piece"):
             nc.sync.dma_start(
-                out=bias_bf[:].rearrange("p (g t) -> p g t", t=4),
+                out=bias[:].rearrange("p (g t) -> p g t", t=4),
                 in_=Wy_b.rearrange("(g p t) -> p g t", p=P, t=4),
             )
         load_w(2)
         load_w(3)
-        load_x(1)
         load_k(0)
         load_k(1)
+        load_x(2)
         load_k(2)
+        load_x(3)
         prior_all = const.tile([P, K_DICT], BF16)
         nc.sync.dma_start(out=prior_all[:], in_=prior.partition_broadcast(P))
 
@@ -88,8 +88,6 @@ def tile_visualdeconfounder_pa_kernel(tc, x, Wy_w, Wy_b, k, prior, out):
 
         ident = const.tile([P, P], F32)
         masks.make_identity(nc, ident[:])
-
-        bias = const.tile([P, 8], F32)
 
         x_codes = keep.tile([P, N_BLOCKS * F_PASSES * P], U32, align_bytes=64)
         x_scales = keep.tile([P, N_BLOCKS * F_PASSES * P], U8, align_bytes=64)
@@ -124,190 +122,235 @@ def tile_visualdeconfounder_pa_kernel(tc, x, Wy_w, Wy_b, k, prior, out):
 
         q_banks = {}
 
-        def first_product(c, a):
+        def first_product(c, i, bank):
             g, h = divmod(c, 2)
             if h == 0:
-                q_banks[g, a] = [
-                    psum.tile([P, 4, P], F32, name="q_bank%d" % b, tag="q", bufs=2) for b in range(2)
-                ]
-            for b in range(2):
-                for s in range(2):
-                    for f in range(F_PASSES):
-                        mx_pass(
-                            q_banks[g, a][b][:, 2 * h + s, :],
-                            w_codes, w_scales, ((2 * c + s) * F_PASSES + f) * P,
-                            x_codes, x_scales, ((2 * a + b) * F_PASSES + f) * P,
-                            P, f, F_PASSES,
-                        )
+                q_banks[g, i] = new_bank(bank)
+            for s in range(2):
+                for f in range(F_PASSES):
+                    mx_pass(
+                        q_banks[g, i][:, 2 * h + s, :],
+                        w_codes, w_scales, ((2 * c + s) * F_PASSES + f) * P,
+                        x_codes, x_scales, (i * F_PASSES + f) * P,
+                        P, f, F_PASSES,
+                    )
 
-        def add_bias(g, a):
-            bias_tn = bias[:, 4 * g : 4 * g + 4].unsqueeze(1).to_broadcast([P, P, 4])
-            for b in range(2):
-                i = 2 * a + b
-                nc.vector.tensor_tensor(
-                    out=q_grouped[g][:, BANK * i : BANK * (i + 1)].rearrange("p (n t) -> p n t", t=4),
-                    in0=q_banks[g, a][b][:].rearrange("p t n -> p n t"),
-                    in1=bias_tn,
-                    op=ALU.add,
-                )
-
-        def quantise_q(g, a):
-            first = BANK * 2 * a
-            quantise(
-                q_grouped[g][:, first : first + 2 * BANK], q_codes, q_scales, g * N_ROWS + 2 * P * a, 2 * P
+        def add_bias(g, i):
+            nc.vector.tensor_tensor(
+                out=q_grouped[g][:, BANK * i : BANK * (i + 1)].rearrange("p (n t) -> p n t", t=4),
+                in0=q_banks[g, i][:].rearrange("p t n -> p n t"),
+                in1=bias[:, 4 * g : 4 * g + 4].unsqueeze(1).to_broadcast([P, P, 4]),
+                op=ALU.add,
             )
 
-        x_units = [
-            (x_raw[a], False, a > 0, x_codes, x_scales, [2 * a * BANK, (2 * a + 1) * BANK])
-            for a in range(2)
-        ]
+        def quantise_q(g, i, blocks):
+            quantise(
+                q_grouped[g][:, BANK * i : BANK * (i + blocks)],
+                q_codes, q_scales, g * N_ROWS + P * i, P * blocks,
+            )
+
+        x_units = [(x_raw[i], 2, False, i > 1, x_codes, x_scales, [i * BANK]) for i in range(N_BLOCKS)]
         w_units = [
-            (w_raw[c], False, c > 0, w_codes, w_scales, [2 * c * BANK, (2 * c + 1) * BANK])
+            (w_raw[c], 4, False, c > 0, w_codes, w_scales, [2 * c * BANK, (2 * c + 1) * BANK])
             for c in range(4)
         ]
         k_units = [
-            (k_raw[c], True, True, k_codes, k_scales, [BANK * c, K_DICT + BANK * c])
+            (k_raw[c], 4, True, True, k_codes, k_scales, [BANK * c, K_DICT + BANK * c])
             for c in range(J_CHUNKS)
         ]
 
-        def split_half(unit, words, h):
-            cols = slice(1024 * h, 1024 * (h + 1))
-            nc.vector.tensor_copy(
-                out=words[:, cols].rearrange("p (g u m) -> p g u m", u=2, m=P),
-                in_=unit[0][:].bitcast(F32)[:, cols].rearrange("p (g m u) -> p g u m", u=2, m=P),
-            )
+        def new_words(unit):
+            if not unit[3]:
+                return unit[0][:].bitcast(F32)
+            split = split_pool.tile([P, UNIT // 2], F32, name="split")
+            return split[:]
 
-        def transpose_unit(unit, words):
+        def split_half(unit, words, h):
+            if unit[3] and h < len(unit[6]):
+                cols = slice(1024 * h, 1024 * (h + 1))
+                nc.vector.tensor_copy(
+                    out=words[:, cols].rearrange("p (g u m) -> p g u m", u=2, m=P),
+                    in_=unit[0][:].bitcast(F32)[:, cols].rearrange("p (g m u) -> p g u m", u=2, m=P),
+                )
+
+        def transpose_unit(unit, words, banks, vector_banks=()):
             grouped = grouped_pool.tile([P, UNIT], BF16, align_bytes=64)
-            order = "p (g b r u) -> p b g r u" if unit[1] else "p (b g r u) -> p b g r u"
-            dest = grouped[:].bitcast(F32).rearrange(order, g=2, b=4, u=2)
-            for b in range(4):
-                bank = psum.tile([P, 4, P], F32, name="t_bank", tag="work")
+            order = "p (g b r u) -> p b g r u" if unit[2] else "p (b g r u) -> p b g r u"
+            dest = grouped[:, : 1024 * unit[1]].bitcast(F32).rearrange(order, g=2, b=unit[1], u=2)
+            for b in range(unit[1]):
+                bank = new_bank(banks[b])
                 for v in range(4):
                     g, u = divmod(v, 2)
                     first = BANK * b + 2 * P * g
-                    if unit[2]:
+                    if unit[3]:
                         plane = words[:, first + P * u : first + P * (u + 1)]
                     else:
                         plane = words[:, first + u : first + 2 * P : 2]
                     nc.tensor.transpose(bank[:, v, :], plane, ident[:])
-                nc.scalar.copy(out=dest[:, b], in_=bank[:].rearrange("p (g u) r -> p g r u", u=2))
+                source = bank[:].rearrange("p (g u) r -> p g r u", u=2)
+                if b in vector_banks:
+                    nc.vector.tensor_copy(out=dest[:, b], in_=source)
+                else:
+                    nc.scalar.copy(out=dest[:, b], in_=source)
             return grouped
 
         def quantise_half(unit, grouped, h):
-            quantise(grouped[:, 2048 * h : 2048 * (h + 1)], unit[3], unit[4], unit[5][h], BANK)
+            if h < len(unit[6]):
+                quantise(grouped[:, 2048 * h : 2048 * (h + 1)], unit[4], unit[5], unit[6][h], BANK)
 
-        steps = [
-            (x_units[0], None),
-            (w_units[0], None),
-            (w_units[1], (0, 0)),
-            (w_units[2], (1, 0)),
-            (w_units[3], (2, 0)),
-            (x_units[1], (3, 0)),
-            (k_units[0], (0, 1)),
-            (k_units[1], (1, 1)),
-            (k_units[2], (2, 1)),
-        ]
-        words = steps[0][0][0][:].bitcast(F32)
-        for j, (unit, product) in enumerate(steps):
-            grouped = transpose_unit(unit, words)
-            if product:
-                first_product(*product)
-            following = steps[j + 1][0] if j + 1 < len(steps) else None
-            if following and following[2]:
-                split = split_pool.tile([P, UNIT // 2], F32, name="split")
-                words = split[:]
-            elif following:
-                words = following[0][:].bitcast(F32)
-            for h in range(2):
-                if following and following[2]:
-                    split_half(following, words, h)
-                quantise_half(unit, grouped, h)
-            if j == 2:
-                nc.vector.tensor_copy(out=bias[:], in_=bias_bf[:])
-            if product and product[0] % 2 == 1:
-                add_bias(product[0] // 2, product[1])
-            if j > 0 and steps[j - 1][1] and steps[j - 1][1][0] % 2 == 1:
-                quantise_q(steps[j - 1][1][0] // 2, steps[j - 1][1][1])
-        first_product(3, 1)
-        add_bias(1, 1)
-        quantise_q(1, 1)
+        s_banks = {}
+        soft_e = [soft.tile([P, K_DICT], F32, name="soft_e%d" % i) for i in range(N_BLOCKS)]
+        result = [soft.tile([P, K_DICT], F32, name="result%d" % i) for i in range(N_BLOCKS)]
+        chunk_max = [small.tile([P, J_CHUNKS], F32, name="chunk_max%d" % i) for i in range(N_BLOCKS)]
+        shift = [small.tile([P, J_CHUNKS], F32, name="shift%d" % i) for i in range(N_BLOCKS)]
+        chunk_sum = [small.tile([P, J_CHUNKS], F32, name="chunk_sum%d" % i) for i in range(N_BLOCKS)]
+        factor = [small.tile([P, J_CHUNKS], F32, name="factor%d" % i) for i in range(N_BLOCKS)]
 
-        def scores(i):
-            banks = []
-            for c in range(J_CHUNKS):
-                in_q = (J_CHUNKS * i + c) % 8 >= 6
-                bank = psum.tile(
-                    [P, BANK], F32, name="s_bank", tag="q" if in_q else "work", bufs=2 if in_q else 6
+        def columns(c):
+            return slice(BANK * c, BANK * (c + 1))
+
+        def open_scores(i, c, bank):
+            s_banks[i, c] = new_bank(bank)
+
+        def score_pass(i, c, g):
+            mx_pass(
+                s_banks[i, c][:].rearrange("p t n -> p (t n)"),
+                q_codes, q_scales, g * N_ROWS + P * i,
+                k_codes, k_scales, g * K_DICT + BANK * c,
+                BANK, g, E_PASSES,
+            )
+
+        def scores(i, c, bank):
+            open_scores(i, c, bank)
+            for g in range(E_PASSES):
+                score_pass(i, c, g)
+
+        def chunk_maximum(i, c):
+            nc.vector.tensor_reduce(
+                out=chunk_max[i][:, c : c + 1],
+                in_=s_banks[i, c][:].rearrange("p t n -> p (t n)"), axis=AXIS.X, op=ALU.max,
+            )
+            nc.vector.tensor_scalar_mul(shift[i][:, c : c + 1], chunk_max[i][:, c : c + 1], -SCALE)
+
+        def exponential(i, c):
+            nc.scalar.activation(
+                out=soft_e[i][:, columns(c)],
+                in_=s_banks[i, c][:].rearrange("p t n -> p (t n)"),
+                func=ACT.Exp,
+                bias=shift[i][:, c : c + 1],
+                scale=SCALE,
+                accum_out=chunk_sum[i][:, c : c + 1],
+            )
+            if c < J_CHUNKS - 1:
+                nc.gpsimd.tensor_tensor(
+                    out=result[i][:, columns(c)],
+                    in0=soft_e[i][:, columns(c)],
+                    in1=prior_all[:, columns(c)],
+                    op=ALU.mult,
                 )
-                for g in range(E_PASSES):
-                    mx_pass(
-                        bank[:],
-                        q_codes, q_scales, g * N_ROWS + P * i,
-                        k_codes, k_scales, g * K_DICT + BANK * c,
-                        BANK, g, E_PASSES,
-                    )
-                banks.append(bank)
-            return banks
 
-        def row_maximum(banks):
-            chunk_max = small.tile([P, J_CHUNKS], F32)
-            for c in range(J_CHUNKS):
-                nc.vector.tensor_reduce(
-                    out=chunk_max[:, c : c + 1], in_=banks[c][:], axis=AXIS.X, op=ALU.max
-                )
-            row_max = small.tile([P, 1], F32)
-            nc.vector.tensor_reduce(out=row_max[:], in_=chunk_max[:], axis=AXIS.X, op=ALU.max)
-            shift = small.tile([P, 1], F32)
-            nc.vector.tensor_scalar_mul(shift[:], row_max[:], -SCALE)
-            return shift
+        def chunk_weights(i):
+            row_shift = small.tile([P, 1], F32)
+            weight = small.tile([P, J_CHUNKS], F32)
+            nc.vector.tensor_reduce(out=row_shift[:], in_=shift[i][:], axis=AXIS.X, op=ALU.min)
+            nc.scalar.activation(
+                out=weight[:], in_=shift[i][:], func=ACT.Exp, bias=row_shift[:], scale=-1.0
+            )
+            return weight
 
-        def exponentials(banks, shift):
-            e = soft.tile([P, K_DICT], F32)
-            result = soft.tile([P, K_DICT], F32)
-            chunk_sum = small.tile([P, J_CHUNKS], F32)
-            for c in range(J_CHUNKS):
-                cols = slice(BANK * c, BANK * (c + 1))
-                nc.scalar.activation(
-                    out=e[:, cols],
-                    in_=banks[c][:],
-                    func=ACT.Exp,
-                    bias=shift[:],
-                    scale=SCALE,
-                    accum_out=chunk_sum[:, c : c + 1],
-                )
-                if c < J_CHUNKS - 1:
-                    nc.gpsimd.tensor_tensor(
-                        out=result[:, cols], in0=e[:, cols], in1=prior_all[:, cols], op=ALU.mult
-                    )
-            return e, result, chunk_sum
-
-        def normalise_and_store(i, e, result, chunk_sum):
-            rows = out[P * i : P * (i + 1), :]
-            first, last = slice(0, K_DICT - BANK), slice(K_DICT - BANK, K_DICT)
+        def chunk_factors(i, weight):
+            weighted = small.tile([P, J_CHUNKS], F32)
             row_sum = small.tile([P, 1], F32)
-            nc.vector.tensor_reduce(out=row_sum[:], in_=chunk_sum[:], axis=AXIS.X, op=ALU.add)
             inverse = small.tile([P, 1], F32)
-            nc.vector.reciprocal(inverse[:], row_sum[:])
             nc.vector.scalar_tensor_tensor(
-                out=result[:, last],
-                in0=e[:, last],
-                scalar=inverse[:],
-                in1=prior_all[:, last],
+                out=weighted[:], in0=weight[:], scalar=1.0, in1=chunk_sum[i][:],
+                op0=ALU.mult, op1=ALU.mult, accum_out=row_sum[:],
+            )
+            nc.vector.reciprocal(inverse[:], row_sum[:])
+            nc.vector.tensor_scalar_mul(factor[i][:], weight[:], inverse[:])
+
+        def normalise_and_store(i):
+            rows = out[P * i : P * (i + 1), :]
+            last = J_CHUNKS - 1
+            nc.vector.scalar_tensor_tensor(
+                out=result[i][:, columns(last)],
+                in0=soft_e[i][:, columns(last)],
+                scalar=factor[i][:, last : last + 1],
+                in1=prior_all[:, columns(last)],
                 op0=ALU.mult,
                 op1=ALU.mult,
             )
-            nc.sync.dma_start(out=rows[:, last], in_=result[:, last])
-            nc.scalar.activation(
-                out=result[:, first], in_=result[:, first], func=ACT.Copy, scale=inverse[:]
-            )
-            nc.sync.dma_start(out=rows[:, first], in_=result[:, first])
+            nc.sync.dma_start(out=rows[:, columns(last)], in_=result[i][:, columns(last)])
+            for c in range(last):
+                nc.scalar.activation(
+                    out=result[i][:, columns(c)], in_=result[i][:, columns(c)],
+                    func=ACT.Copy, scale=factor[i][:, c : c + 1],
+                )
+            nc.sync.dma_start(out=rows[:, : BANK * last], in_=result[i][:, : BANK * last])
 
-        pending = None
-        for i in range(N_BLOCKS):
-            banks = scores(i)
-            started = exponentials(banks, row_maximum(banks))
-            if pending:
-                normalise_and_store(i - 1, *pending)
-            pending = started
-        normalise_and_store(N_BLOCKS - 1, *pending)
+        units = x_units[:2] + w_units + k_units[:2] + [x_units[2], k_units[2], x_units[3]]
+        unit_banks = [[0, 1], [2, 3]] + [[0, 1, 2, 3]] * 6 + [[0, 1], [2, 0, 1, 2], [0, 1]]
+        products = {
+            3: [(0, 0, 4), (0, 1, 5)],
+            4: [(1, 0, 4), (1, 1, 5)],
+            5: [(2, 0, 4), (2, 1, 5)],
+            6: [(3, 0, 4), (3, 1, 5)],
+            9: [(0, 2, 4), (1, 2, 4)],
+            10: [(2, 2, 2), (3, 2, 2)],
+            11: [(0, 3, 0), (1, 3, 0)],
+            12: [(2, 3, 1), (3, 3, 1)],
+        }
+        chunks = {
+            8: [(0, 0, 6), (1, 0, 7)],
+            9: [(0, 1, 3), (1, 1, 5)],
+            10: [(0, 2, 6), (1, 2, 7)],
+            11: [(2, 0, 3), (2, 1, 5), (2, 2, 4)],
+            13: [(3, 0, 6), (3, 1, 7), (3, 2, 2)],
+        }
+
+        def finished_q(j):
+            return [(c // 2, i) for c, i, bank in products.get(j, []) if c % 2 == 1]
+
+        weights = {}
+
+        def step(j, words):
+            unit = units[j] if j < len(units) else None
+            following = units[j + 1] if j + 1 < len(units) else None
+            next_words = new_words(following) if following else None
+            if unit:
+                grouped = transpose_unit(unit, words, unit_banks[j], (1,) if j < 2 else ())
+            for g, i in finished_q(j - 1):
+                add_bias(g, i)
+            if following:
+                split_half(following, next_words, 0)
+            for i, c, bank in chunks.get(j - 1, []):
+                chunk_maximum(i, c)
+                exponential(i, c)
+            for g, i in finished_q(j - 1):
+                quantise_q(g, i, 1)
+            if unit:
+                quantise_half(unit, grouped, 0)
+            if following:
+                split_half(following, next_words, 1)
+            if unit:
+                quantise_half(unit, grouped, 1)
+            for i in sorted(weights):
+                chunk_factors(i, weights.pop(i))
+                normalise_and_store(i)
+            for i, c, bank in chunks.get(j - 1, []):
+                if c == J_CHUNKS - 1:
+                    weights[i] = chunk_weights(i)
+            for product in products.get(j, []):
+                first_product(*product)
+            for i, c, bank in chunks.get(j, []):
+                scores(i, c, bank)
+            return next_words
+
+        words = new_words(units[0])
+        with tc.manual_schedule():
+            for j in range(3):
+                words = step(j, words)
+        for j in range(3, 15):
+            words = step(j, words)
+        chunk_factors(3, weights[3])
+        normalise_and_store(3)

@@ -149,13 +149,13 @@ def tile_visualdeconfounder_pa_kernel(tc, x, Wy_w, Wy_b, k, prior, out):
                 q_codes, q_scales, g * N_ROWS + P * i, P * blocks,
             )
 
-        x_units = [(x_raw[i], 2, False, i > 1, x_codes, x_scales, [i * BANK]) for i in range(N_BLOCKS)]
+        x_units = [(x_raw[i], 2, False, False, x_codes, x_scales, [i * BANK]) for i in range(N_BLOCKS)]
         w_units = [
-            (w_raw[c], 4, False, c > 0, w_codes, w_scales, [2 * c * BANK, (2 * c + 1) * BANK])
+            (w_raw[c], 4, False, c > 1, w_codes, w_scales, [2 * c * BANK, (2 * c + 1) * BANK])
             for c in range(4)
         ]
         k_units = [
-            (k_raw[c], 4, True, True, k_codes, k_scales, [BANK * c, K_DICT + BANK * c])
+            (k_raw[c], 4, True, c < 2, k_codes, k_scales, [BANK * c, K_DICT + BANK * c])
             for c in range(J_CHUNKS)
         ]
 
@@ -232,6 +232,8 @@ def tile_visualdeconfounder_pa_kernel(tc, x, Wy_w, Wy_b, k, prior, out):
             )
             nc.vector.tensor_scalar_mul(shift[i][:, c : c + 1], chunk_max[i][:, c : c + 1], -SCALE)
 
+        finish = ["SSV", "SSV", "SVV", "SWV"]
+
         def exponential(i, c):
             nc.scalar.activation(
                 out=soft_e[i][:, columns(c)],
@@ -241,7 +243,7 @@ def tile_visualdeconfounder_pa_kernel(tc, x, Wy_w, Wy_b, k, prior, out):
                 scale=SCALE,
                 accum_out=chunk_sum[i][:, c : c + 1],
             )
-            if c < J_CHUNKS - 1:
+            if finish[i][c] != "V":
                 nc.gpsimd.tensor_tensor(
                     out=result[i][:, columns(c)],
                     in0=soft_e[i][:, columns(c)],
@@ -270,23 +272,19 @@ def tile_visualdeconfounder_pa_kernel(tc, x, Wy_w, Wy_b, k, prior, out):
             nc.vector.tensor_scalar_mul(factor[i][:], weight[:], inverse[:])
 
         def normalise_and_store(i):
-            rows = out[P * i : P * (i + 1), :]
-            last = J_CHUNKS - 1
-            nc.vector.scalar_tensor_tensor(
-                out=result[i][:, columns(last)],
-                in0=soft_e[i][:, columns(last)],
-                scalar=factor[i][:, last : last + 1],
-                in1=prior_all[:, columns(last)],
-                op0=ALU.mult,
-                op1=ALU.mult,
-            )
-            nc.sync.dma_start(out=rows[:, columns(last)], in_=result[i][:, columns(last)])
-            for c in range(last):
-                nc.scalar.activation(
-                    out=result[i][:, columns(c)], in_=result[i][:, columns(c)],
-                    func=ACT.Copy, scale=factor[i][:, c : c + 1],
-                )
-            nc.sync.dma_start(out=rows[:, : BANK * last], in_=result[i][:, : BANK * last])
+            for c in range(J_CHUNKS):
+                part = result[i][:, columns(c)]
+                f = factor[i][:, c : c + 1]
+                if finish[i][c] == "S":
+                    nc.scalar.activation(out=part, in_=part, func=ACT.Copy, scale=f)
+                elif finish[i][c] == "W":
+                    nc.vector.tensor_scalar_mul(part, part, f)
+                else:
+                    nc.vector.scalar_tensor_tensor(
+                        out=part, in0=soft_e[i][:, columns(c)], scalar=f, in1=prior_all[:, columns(c)],
+                        op0=ALU.mult, op1=ALU.mult,
+                    )
+                nc.sync.dma_start(out=out[P * i : P * (i + 1), columns(c)], in_=part)
 
         units = x_units[:2] + w_units + k_units[:2] + [x_units[2], k_units[2], x_units[3]]
         unit_banks = [[0, 1], [2, 3]] + [[0, 1, 2, 3]] * 6 + [[0, 1], [2, 0, 1, 2], [0, 1]]
@@ -342,15 +340,24 @@ def tile_visualdeconfounder_pa_kernel(tc, x, Wy_w, Wy_b, k, prior, out):
                     weights[i] = chunk_weights(i)
             for product in products.get(j, []):
                 first_product(*product)
-            for i, c, bank in chunks.get(j, []):
-                scores(i, c, bank)
+            if j < 12:
+                for i, c, bank in chunks.get(j, []):
+                    scores(i, c, bank)
+            if j == 12:
+                for i, c, bank in chunks[13]:
+                    open_scores(i, c, bank)
+                    score_pass(i, c, 0)
+            if j == 13:
+                for i, c, bank in chunks[13]:
+                    score_pass(i, c, 1)
             return next_words
 
         words = new_words(units[0])
         with tc.manual_schedule():
             for j in range(3):
                 words = step(j, words)
-        for j in range(3, 15):
-            words = step(j, words)
-        chunk_factors(3, weights[3])
-        normalise_and_store(3)
+        with tc.manual_schedule(engines={mybir.EngineType.PE}):
+            for j in range(3, 15):
+                words = step(j, words)
+            chunk_factors(3, weights[3])
+            normalise_and_store(3)

@@ -28,6 +28,7 @@ FLOPS = 2 * N_ROWS * F_DIM * E_DIM + 2 * N_ROWS * E_DIM * K_DICT
 def tile_visualdeconfounder_pa_kernel(tc, x, Wy_w, Wy_b, k, prior, out):
     nc = tc.nc
     with ExitStack() as ctx:
+        ctx.enter_context(tc.manual_schedule())
         const = ctx.enter_context(tc.tile_pool(name="const", bufs=1))
         raw_pool = ctx.enter_context(tc.tile_pool(name="raw", bufs=1))
         keep = ctx.enter_context(tc.tile_pool(name="keep", bufs=1))
@@ -47,16 +48,18 @@ def tile_visualdeconfounder_pa_kernel(tc, x, Wy_w, Wy_b, k, prior, out):
         def load_w(c):
             g, h = divmod(c, 2)
             rows = Wy_w[512 * g : 512 * (g + 1), :].rearrange("(p t) f -> p t f", t=4)
-            nc.sync.dma_start(
-                out=w_raw[c][:].rearrange("p (s f) -> p s f", s=2), in_=rows[:, 2 * h : 2 * h + 2, :]
-            )
+            for s in range(2):
+                nc.sync.dma_start(
+                    out=w_raw[c][:, F_DIM * s : F_DIM * (s + 1)], in_=rows[:, 2 * h + s, :]
+                )
 
         def load_k(c):
-            rows = k[BANK * c : BANK * (c + 1), :]
-            nc.sync.dma_start(
-                out=k_raw[c][:].rearrange("p (b e) -> p b e", b=4),
-                in_=rows.rearrange("(b p) e -> p b e", p=P),
-            )
+            for half in range(2):
+                first = BANK * c + 2 * P * half
+                nc.sync.dma_start(
+                    out=k_raw[c][:, 2048 * half : 2048 * (half + 1)].rearrange("p (b e) -> p b e", b=2),
+                    in_=k[first : first + 2 * P, :].rearrange("(b p) e -> p b e", p=P),
+                )
 
         def load_x(i):
             nc.sync.dma_start(out=x_raw[i][:], in_=x[P * i : P * (i + 1), :])
@@ -230,11 +233,13 @@ def tile_visualdeconfounder_pa_kernel(tc, x, Wy_w, Wy_b, k, prior, out):
                 out=chunk_max[i][:, c : c + 1],
                 in_=s_banks[i, c][:].rearrange("p t n -> p (t n)"), axis=AXIS.X, op=ALU.max,
             )
-            nc.vector.tensor_scalar_mul(shift[i][:, c : c + 1], chunk_max[i][:, c : c + 1], -SCALE)
 
-        finish = ["SSV", "SSV", "SVV", "SWV"]
+        finish = ["SSV", "SSV", "VVV", "VVV"]
 
         def exponential(i, c):
+            nc.scalar.activation(
+                out=shift[i][:, c : c + 1], in_=chunk_max[i][:, c : c + 1], func=ACT.Copy, scale=-SCALE
+            )
             nc.scalar.activation(
                 out=soft_e[i][:, columns(c)],
                 in_=s_banks[i, c][:].rearrange("p t n -> p (t n)"),
@@ -260,16 +265,21 @@ def tile_visualdeconfounder_pa_kernel(tc, x, Wy_w, Wy_b, k, prior, out):
             )
             return weight
 
-        def chunk_factors(i, weight):
-            weighted = small.tile([P, J_CHUNKS], F32)
-            row_sum = small.tile([P, 1], F32)
-            inverse = small.tile([P, 1], F32)
-            nc.vector.scalar_tensor_tensor(
-                out=weighted[:], in0=weight[:], scalar=1.0, in1=chunk_sum[i][:],
-                op0=ALU.mult, op1=ALU.mult, accum_out=row_sum[:],
-            )
-            nc.vector.reciprocal(inverse[:], row_sum[:])
-            nc.vector.tensor_scalar_mul(factor[i][:], weight[:], inverse[:])
+        def chunk_factors(blocks):
+            row_sum = {}
+            inverse = {}
+            for i in blocks:
+                weighted = small.tile([P, J_CHUNKS], F32)
+                row_sum[i] = small.tile([P, 1], F32, name="row_sum")
+                nc.vector.scalar_tensor_tensor(
+                    out=weighted[:], in0=weights[i][:], scalar=1.0, in1=chunk_sum[i][:],
+                    op0=ALU.mult, op1=ALU.mult, accum_out=row_sum[i][:],
+                )
+            for i in blocks:
+                inverse[i] = small.tile([P, 1], F32, name="inverse")
+                nc.vector.reciprocal(inverse[i][:], row_sum[i][:])
+            for i in blocks:
+                nc.vector.tensor_scalar_mul(factor[i][:], weights[i][:], inverse[i][:])
 
         def normalise_and_store(i):
             for c in range(J_CHUNKS):
@@ -310,6 +320,7 @@ def tile_visualdeconfounder_pa_kernel(tc, x, Wy_w, Wy_b, k, prior, out):
             return [(c // 2, i) for c, i, bank in products.get(j, []) if c % 2 == 1]
 
         weights = {}
+        NORM = {13: [0, 1], 14: [2]}
 
         def step(j, words):
             unit = units[j] if j < len(units) else None
@@ -332,8 +343,8 @@ def tile_visualdeconfounder_pa_kernel(tc, x, Wy_w, Wy_b, k, prior, out):
                 split_half(following, next_words, 1)
             if unit:
                 quantise_half(unit, grouped, 1)
-            for i in sorted(weights):
-                chunk_factors(i, weights.pop(i))
+            chunk_factors(NORM.get(j, []))
+            for i in NORM.get(j, []):
                 normalise_and_store(i)
             for i, c, bank in chunks.get(j - 1, []):
                 if c == J_CHUNKS - 1:
@@ -353,11 +364,7 @@ def tile_visualdeconfounder_pa_kernel(tc, x, Wy_w, Wy_b, k, prior, out):
             return next_words
 
         words = new_words(units[0])
-        with tc.manual_schedule():
-            for j in range(3):
-                words = step(j, words)
-        with tc.manual_schedule(engines={mybir.EngineType.PE}):
-            for j in range(3, 15):
-                words = step(j, words)
-            chunk_factors(3, weights[3])
-            normalise_and_store(3)
+        for j in range(15):
+            words = step(j, words)
+        chunk_factors([3])
+        normalise_and_store(3)

@@ -205,6 +205,7 @@ def tile_visualdeconfounder_pa_kernel(tc, x, Wy_w, Wy_b, k, prior, out):
         soft_e = [soft.tile([P, K_DICT], F32, name="soft_e%d" % i) for i in range(N_BLOCKS)]
         result = [soft.tile([P, K_DICT], F32, name="result%d" % i) for i in range(N_BLOCKS)]
         chunk_max = [small.tile([P, J_CHUNKS], F32, name="chunk_max%d" % i) for i in range(N_BLOCKS)]
+        row_max = [small.tile([P, 1], F32, name="row_max%d" % i) for i in range(N_BLOCKS)]
         shift = [small.tile([P, J_CHUNKS], F32, name="shift%d" % i) for i in range(N_BLOCKS)]
         chunk_sum = [small.tile([P, J_CHUNKS], F32, name="chunk_sum%d" % i) for i in range(N_BLOCKS)]
         factor = [small.tile([P, J_CHUNKS], F32, name="factor%d" % i) for i in range(N_BLOCKS)]
@@ -236,10 +237,15 @@ def tile_visualdeconfounder_pa_kernel(tc, x, Wy_w, Wy_b, k, prior, out):
 
         finish = ["SSV", "SSV", "VVV", "VVV"]
 
-        def exponential(i, c):
+        def row_maximum(i):
+            nc.vector.tensor_reduce(out=row_max[i][:], in_=chunk_max[i][:], axis=AXIS.X, op=ALU.max)
+
+        def shifts(i, c):
             nc.scalar.activation(
                 out=shift[i][:, c : c + 1], in_=chunk_max[i][:, c : c + 1], func=ACT.Copy, scale=-SCALE
             )
+
+        def exponential(i, c):
             nc.scalar.activation(
                 out=soft_e[i][:, columns(c)],
                 in_=s_banks[i, c][:].rearrange("p t n -> p (t n)"),
@@ -259,9 +265,9 @@ def tile_visualdeconfounder_pa_kernel(tc, x, Wy_w, Wy_b, k, prior, out):
         def chunk_weights(i):
             row_shift = small.tile([P, 1], F32)
             weight = small.tile([P, J_CHUNKS], F32)
-            nc.vector.tensor_reduce(out=row_shift[:], in_=shift[i][:], axis=AXIS.X, op=ALU.min)
+            nc.scalar.activation(out=row_shift[:], in_=row_max[i][:], func=ACT.Copy, scale=-SCALE)
             nc.scalar.activation(
-                out=weight[:], in_=shift[i][:], func=ACT.Exp, bias=row_shift[:], scale=-1.0
+                out=weight[:], in_=chunk_max[i][:], func=ACT.Exp, bias=row_shift[:], scale=SCALE
             )
             return weight
 
@@ -320,7 +326,8 @@ def tile_visualdeconfounder_pa_kernel(tc, x, Wy_w, Wy_b, k, prior, out):
             return [(c // 2, i) for c, i, bank in products.get(j, []) if c % 2 == 1]
 
         weights = {}
-        NORM = {13: [0, 1], 14: [2]}
+
+        finished = {12: [0, 1], 13: [2]}
 
         def step(j, words):
             unit = units[j] if j < len(units) else None
@@ -328,24 +335,10 @@ def tile_visualdeconfounder_pa_kernel(tc, x, Wy_w, Wy_b, k, prior, out):
             next_words = new_words(following) if following else None
             if unit:
                 grouped = transpose_unit(unit, words, unit_banks[j], (1,) if j < 2 else ())
-            for g, i in finished_q(j - 1):
-                add_bias(g, i)
-            if following:
-                split_half(following, next_words, 0)
             for i, c, bank in chunks.get(j - 1, []):
-                chunk_maximum(i, c)
+                shifts(i, c)
+            for i, c, bank in chunks.get(j - 1, []):
                 exponential(i, c)
-            for g, i in finished_q(j - 1):
-                quantise_q(g, i, 1)
-            if unit:
-                quantise_half(unit, grouped, 0)
-            if following:
-                split_half(following, next_words, 1)
-            if unit:
-                quantise_half(unit, grouped, 1)
-            chunk_factors(NORM.get(j, []))
-            for i in NORM.get(j, []):
-                normalise_and_store(i)
             for i, c, bank in chunks.get(j - 1, []):
                 if c == J_CHUNKS - 1:
                     weights[i] = chunk_weights(i)
@@ -361,6 +354,29 @@ def tile_visualdeconfounder_pa_kernel(tc, x, Wy_w, Wy_b, k, prior, out):
             if j == 13:
                 for i, c, bank in chunks[13]:
                     score_pass(i, c, 1)
+            ready = finished_q(j)
+            if following:
+                for h in range(2):
+                    split_half(following, next_words, h)
+            if unit:
+                if unit[2] and j == 6:
+                    for g, i in ready[:1]:
+                        add_bias(g, i)
+                    ready = ready[1:]
+                for h in range(2):
+                    quantise_half(unit, grouped, h)
+            for g, i in ready:
+                add_bias(g, i)
+            for i, c, bank in chunks.get(j, []):
+                chunk_maximum(i, c)
+            for g, i in finished_q(j):
+                quantise_q(g, i, 1)
+            for i, c, bank in chunks.get(j, []):
+                if c == J_CHUNKS - 1:
+                    row_maximum(i)
+            chunk_factors(finished.get(j, []))
+            for i in finished.get(j, []):
+                normalise_and_store(i)
             return next_words
 
         words = new_words(units[0])

@@ -1,4 +1,5 @@
 from contextlib import ExitStack
+from functools import partial
 
 import concourse.masks as masks
 import concourse.mybir as mybir
@@ -271,21 +272,21 @@ def tile_visualdeconfounder_pa_kernel(tc, x, Wy_w, Wy_b, k, prior, out):
             )
             return weight
 
-        def chunk_factors(blocks):
-            row_sum = {}
-            inverse = {}
-            for i in blocks:
-                weighted = small.tile([P, J_CHUNKS], F32)
-                row_sum[i] = small.tile([P, 1], F32, name="row_sum")
-                nc.vector.scalar_tensor_tensor(
-                    out=weighted[:], in0=weights[i][:], scalar=1.0, in1=chunk_sum[i][:],
-                    op0=ALU.mult, op1=ALU.mult, accum_out=row_sum[i][:],
-                )
-            for i in blocks:
-                inverse[i] = small.tile([P, 1], F32, name="inverse")
-                nc.vector.reciprocal(inverse[i][:], row_sum[i][:])
-            for i in blocks:
-                nc.vector.tensor_scalar_mul(factor[i][:], weights[i][:], inverse[i][:])
+        row_sum = [small.tile([P, 1], F32, name="row_sum%d" % i) for i in range(N_BLOCKS)]
+        inverse = [small.tile([P, 1], F32, name="inverse%d" % i) for i in range(N_BLOCKS)]
+
+        def row_total(i):
+            weighted = small.tile([P, J_CHUNKS], F32)
+            nc.vector.scalar_tensor_tensor(
+                out=weighted[:], in0=weights[i][:], scalar=1.0, in1=chunk_sum[i][:],
+                op0=ALU.mult, op1=ALU.mult, accum_out=row_sum[i][:],
+            )
+
+        def invert(i):
+            nc.vector.reciprocal(inverse[i][:], row_sum[i][:])
+
+        def factors(i):
+            nc.vector.tensor_scalar_mul(factor[i][:], weights[i][:], inverse[i][:])
 
         def normalise_and_store(i):
             for c in range(J_CHUNKS):
@@ -303,23 +304,25 @@ def tile_visualdeconfounder_pa_kernel(tc, x, Wy_w, Wy_b, k, prior, out):
                 nc.sync.dma_start(out=out[P * i : P * (i + 1), columns(c)], in_=part)
 
         units = x_units[:2] + w_units + k_units[:2] + [x_units[2], k_units[2], x_units[3]]
-        unit_banks = [[0, 1], [2, 3]] + [[0, 1, 2, 3]] * 6 + [[0, 1], [2, 0, 1, 2], [0, 1]]
+        unit_banks = [
+            [0, 1], [2, 3], [4, 5, 6, 7], [0, 1, 2, 3], [6, 7, 0, 1], [2, 3, 6, 7],
+            [4, 5, 2, 3], [6, 7, 4, 5], [2, 3], [0, 1, 4, 5], [0, 1],
+        ]
         products = {
             3: [(0, 0, 4), (0, 1, 5)],
             4: [(1, 0, 4), (1, 1, 5)],
-            5: [(2, 0, 4), (2, 1, 5)],
-            6: [(3, 0, 4), (3, 1, 5)],
-            9: [(0, 2, 4), (1, 2, 4)],
-            10: [(2, 2, 2), (3, 2, 2)],
+            5: [(2, 0, 0), (2, 1, 1)],
+            6: [(3, 0, 0), (3, 1, 1)],
+            10: [(0, 2, 4), (1, 2, 4), (2, 2, 5), (3, 2, 5)],
             11: [(0, 3, 0), (1, 3, 0)],
             12: [(2, 3, 1), (3, 3, 1)],
         }
         chunks = {
             8: [(0, 0, 6), (1, 0, 7)],
-            9: [(0, 1, 3), (1, 1, 5)],
+            9: [(0, 1, 2), (1, 1, 3)],
             10: [(0, 2, 6), (1, 2, 7)],
-            11: [(2, 0, 3), (2, 1, 5), (2, 2, 4)],
-            13: [(3, 0, 6), (3, 1, 7), (3, 2, 2)],
+            11: [(2, 0, 2), (2, 1, 3), (2, 2, 4)],
+            13: [(3, 0, 6), (3, 1, 7), (3, 2, 5)],
         }
 
         def finished_q(j):
@@ -327,7 +330,7 @@ def tile_visualdeconfounder_pa_kernel(tc, x, Wy_w, Wy_b, k, prior, out):
 
         weights = {}
 
-        finished = {12: [0, 1], 13: [2]}
+        closing = {12: [0, 1], 13: [2]}
 
         def step(j, words):
             unit = units[j] if j < len(units) else None
@@ -354,33 +357,36 @@ def tile_visualdeconfounder_pa_kernel(tc, x, Wy_w, Wy_b, k, prior, out):
             if j == 13:
                 for i, c, bank in chunks[13]:
                     score_pass(i, c, 1)
-            ready = finished_q(j)
             if following:
                 for h in range(2):
                     split_half(following, next_words, h)
-            if unit:
-                if unit[2] and j == 6:
-                    for g, i in ready[:1]:
-                        add_bias(g, i)
-                    ready = ready[1:]
-                for h in range(2):
-                    quantise_half(unit, grouped, h)
-            for g, i in ready:
-                add_bias(g, i)
+            quantising = [partial(quantise_half, unit, grouped, h) for h in range(2)] if unit else []
+            biasing = [partial(add_bias, g, i) for g, i in finished_q(j)]
+            if unit and unit[2]:
+                work = biasing[:1] + quantising + biasing[1:]
+            else:
+                work = quantising[:1] + biasing[:1] + quantising[1:] + biasing[1:]
+            for task in work:
+                task()
             for i, c, bank in chunks.get(j, []):
                 chunk_maximum(i, c)
+            for i in closing.get(j, []):
+                row_total(i)
             for g, i in finished_q(j):
                 quantise_q(g, i, 1)
             for i, c, bank in chunks.get(j, []):
                 if c == J_CHUNKS - 1:
                     row_maximum(i)
-            chunk_factors(finished.get(j, []))
-            for i in finished.get(j, []):
+            for short in (invert, factors):
+                for i in closing.get(j, []):
+                    short(i)
+            for i in closing.get(j, []):
                 normalise_and_store(i)
             return next_words
 
         words = new_words(units[0])
         for j in range(15):
             words = step(j, words)
-        chunk_factors([3])
+        for short in (row_total, invert, factors):
+            short(3)
         normalise_and_store(3)

@@ -207,6 +207,7 @@ def tile_visualdeconfounder_pa_kernel(tc, x, Wy_w, Wy_b, k, prior, out):
         result = [soft.tile([P, K_DICT], F32, name="result%d" % i) for i in range(N_BLOCKS)]
         chunk_max = [small.tile([P, J_CHUNKS], F32, name="chunk_max%d" % i) for i in range(N_BLOCKS)]
         row_max = [small.tile([P, 1], F32, name="row_max%d" % i) for i in range(N_BLOCKS)]
+        row_shift = [small.tile([P, 1], F32, name="row_shift%d" % i) for i in range(N_BLOCKS)]
         shift = [small.tile([P, J_CHUNKS], F32, name="shift%d" % i) for i in range(N_BLOCKS)]
         chunk_sum = [small.tile([P, J_CHUNKS], F32, name="chunk_sum%d" % i) for i in range(N_BLOCKS)]
         factor = [small.tile([P, J_CHUNKS], F32, name="factor%d" % i) for i in range(N_BLOCKS)]
@@ -236,26 +237,25 @@ def tile_visualdeconfounder_pa_kernel(tc, x, Wy_w, Wy_b, k, prior, out):
                 in_=s_banks[i, c][:].rearrange("p t n -> p (t n)"), axis=AXIS.X, op=ALU.max,
             )
 
-        finish = ["SSV", "SSV", "VVV", "VVV"]
+        def by_gpsimd(i, c):
+            return i < 2 and c < J_CHUNKS - 1
 
         def row_maximum(i):
             nc.vector.tensor_reduce(out=row_max[i][:], in_=chunk_max[i][:], axis=AXIS.X, op=ALU.max)
 
-        def shifts(i, c):
-            nc.scalar.activation(
-                out=shift[i][:, c : c + 1], in_=chunk_max[i][:, c : c + 1], func=ACT.Copy, scale=-SCALE
-            )
+        def negated(out, maxima):
+            nc.scalar.activation(out=out, in_=maxima, func=ACT.Copy, scale=-SCALE)
 
-        def exponential(i, c):
+        def exponential(i, c, bias):
             nc.scalar.activation(
                 out=soft_e[i][:, columns(c)],
                 in_=s_banks[i, c][:].rearrange("p t n -> p (t n)"),
                 func=ACT.Exp,
-                bias=shift[i][:, c : c + 1],
+                bias=bias,
                 scale=SCALE,
                 accum_out=chunk_sum[i][:, c : c + 1],
             )
-            if finish[i][c] != "V":
+            if by_gpsimd(i, c):
                 nc.gpsimd.tensor_tensor(
                     out=result[i][:, columns(c)],
                     in0=soft_e[i][:, columns(c)],
@@ -263,45 +263,63 @@ def tile_visualdeconfounder_pa_kernel(tc, x, Wy_w, Wy_b, k, prior, out):
                     op=ALU.mult,
                 )
 
+        def exponentials(scored):
+            for i, c, bank in scored:
+                negated(shift[i][:, c : c + 1], chunk_max[i][:, c : c + 1])
+            for i, c, bank in scored:
+                exponential(i, c, shift[i][:, c : c + 1])
+
+        def whole_row(i):
+            negated(row_shift[i][:], row_max[i][:])
+            for c in range(J_CHUNKS):
+                exponential(i, c, row_shift[i][:])
+
         def chunk_weights(i):
-            row_shift = small.tile([P, 1], F32)
             weight = small.tile([P, J_CHUNKS], F32)
-            nc.scalar.activation(out=row_shift[:], in_=row_max[i][:], func=ACT.Copy, scale=-SCALE)
+            negated(row_shift[i][:], row_max[i][:])
             nc.scalar.activation(
-                out=weight[:], in_=chunk_max[i][:], func=ACT.Exp, bias=row_shift[:], scale=SCALE
+                out=weight[:], in_=chunk_max[i][:], func=ACT.Exp, bias=row_shift[i][:], scale=SCALE
             )
             return weight
 
         row_sum = [small.tile([P, 1], F32, name="row_sum%d" % i) for i in range(N_BLOCKS)]
         inverse = [small.tile([P, 1], F32, name="inverse%d" % i) for i in range(N_BLOCKS)]
 
-        def row_total(i):
+        def weighted_total(i):
             weighted = small.tile([P, J_CHUNKS], F32)
             nc.vector.scalar_tensor_tensor(
                 out=weighted[:], in0=weights[i][:], scalar=1.0, in1=chunk_sum[i][:],
                 op0=ALU.mult, op1=ALU.mult, accum_out=row_sum[i][:],
             )
 
+        def total(i):
+            nc.vector.tensor_reduce(out=row_sum[i][:], in_=chunk_sum[i][:], axis=AXIS.X, op=ALU.add)
+
         def invert(i):
             nc.vector.reciprocal(inverse[i][:], row_sum[i][:])
 
-        def factors(i):
-            nc.vector.tensor_scalar_mul(factor[i][:], weights[i][:], inverse[i][:])
+        def store(i, c):
+            nc.sync.dma_start(out=out[P * i : P * (i + 1), columns(c)], in_=result[i][:, columns(c)])
 
-        def normalise_and_store(i):
+        def finish_by_scalar(i):
             for c in range(J_CHUNKS):
-                part = result[i][:, columns(c)]
-                f = factor[i][:, c : c + 1]
-                if finish[i][c] == "S":
-                    nc.scalar.activation(out=part, in_=part, func=ACT.Copy, scale=f)
-                elif finish[i][c] == "W":
-                    nc.vector.tensor_scalar_mul(part, part, f)
-                else:
+                if by_gpsimd(i, c):
+                    part = result[i][:, columns(c)]
+                    nc.scalar.activation(out=part, in_=part, func=ACT.Copy, scale=factor[i][:, c : c + 1])
+                    store(i, c)
+
+        def finish_by_vector(i):
+            for c in range(J_CHUNKS):
+                if not by_gpsimd(i, c):
                     nc.vector.scalar_tensor_tensor(
-                        out=part, in0=soft_e[i][:, columns(c)], scalar=f, in1=prior_all[:, columns(c)],
-                        op0=ALU.mult, op1=ALU.mult,
+                        out=result[i][:, columns(c)],
+                        in0=soft_e[i][:, columns(c)],
+                        scalar=factor[i][:, c : c + 1] if i < 2 else inverse[i][:],
+                        in1=prior_all[:, columns(c)],
+                        op0=ALU.mult,
+                        op1=ALU.mult,
                     )
-                nc.sync.dma_start(out=out[P * i : P * (i + 1), columns(c)], in_=part)
+                    store(i, c)
 
         units = x_units[:2] + w_units + k_units[:2] + [x_units[2], k_units[2], x_units[3]]
         unit_banks = [
@@ -314,55 +332,32 @@ def tile_visualdeconfounder_pa_kernel(tc, x, Wy_w, Wy_b, k, prior, out):
             5: [(2, 0, 0), (2, 1, 1)],
             6: [(3, 0, 0), (3, 1, 1)],
             10: [(0, 2, 4), (1, 2, 4), (2, 2, 5), (3, 2, 5)],
-            11: [(0, 3, 0), (1, 3, 0)],
-            12: [(2, 3, 1), (3, 3, 1)],
         }
         chunks = {
             8: [(0, 0, 6), (1, 0, 7)],
             9: [(0, 1, 2), (1, 1, 3)],
             10: [(0, 2, 6), (1, 2, 7)],
-            11: [(2, 0, 2), (2, 1, 3), (2, 2, 4)],
-            13: [(3, 0, 6), (3, 1, 7), (3, 2, 5)],
         }
 
         def finished_q(j):
             return [(c // 2, i) for c, i, bank in products.get(j, []) if c % 2 == 1]
 
-        weights = {}
-
-        closing = {12: [0, 1], 13: [2]}
-
         def step(j, words):
-            unit = units[j] if j < len(units) else None
+            unit = units[j]
             following = units[j + 1] if j + 1 < len(units) else None
             next_words = new_words(following) if following else None
-            if unit:
-                grouped = transpose_unit(unit, words, unit_banks[j], (1,) if j < 2 else ())
-            for i, c, bank in chunks.get(j - 1, []):
-                shifts(i, c)
-            for i, c, bank in chunks.get(j - 1, []):
-                exponential(i, c)
-            for i, c, bank in chunks.get(j - 1, []):
-                if c == J_CHUNKS - 1:
-                    weights[i] = chunk_weights(i)
+            grouped = transpose_unit(unit, words, unit_banks[j], (1,) if j < 2 else ())
+            exponentials(chunks.get(j - 1, []))
             for product in products.get(j, []):
                 first_product(*product)
-            if j < 12:
-                for i, c, bank in chunks.get(j, []):
-                    scores(i, c, bank)
-            if j == 12:
-                for i, c, bank in chunks[13]:
-                    open_scores(i, c, bank)
-                    score_pass(i, c, 0)
-            if j == 13:
-                for i, c, bank in chunks[13]:
-                    score_pass(i, c, 1)
+            for i, c, bank in chunks.get(j, []):
+                scores(i, c, bank)
             if following:
                 for h in range(2):
                     split_half(following, next_words, h)
-            quantising = [partial(quantise_half, unit, grouped, h) for h in range(2)] if unit else []
+            quantising = [partial(quantise_half, unit, grouped, h) for h in range(2)]
             biasing = [partial(add_bias, g, i) for g, i in finished_q(j)]
-            if unit and unit[2]:
+            if unit[2]:
                 work = biasing[:1] + quantising + biasing[1:]
             else:
                 work = quantising[:1] + biasing[:1] + quantising[1:] + biasing[1:]
@@ -370,23 +365,55 @@ def tile_visualdeconfounder_pa_kernel(tc, x, Wy_w, Wy_b, k, prior, out):
                 task()
             for i, c, bank in chunks.get(j, []):
                 chunk_maximum(i, c)
-            for i in closing.get(j, []):
-                row_total(i)
             for g, i in finished_q(j):
                 quantise_q(g, i, 1)
-            for i, c, bank in chunks.get(j, []):
-                if c == J_CHUNKS - 1:
-                    row_maximum(i)
-            for short in (invert, factors):
-                for i in closing.get(j, []):
-                    short(i)
-            for i in closing.get(j, []):
-                normalise_and_store(i)
             return next_words
 
         words = new_words(units[0])
-        for j in range(15):
+        for j in range(len(units)):
             words = step(j, words)
-        for short in (row_total, invert, factors):
-            short(3)
-        normalise_and_store(3)
+
+        for i in range(2):
+            row_maximum(i)
+        exponentials(chunks[10])
+        weights = [chunk_weights(i) for i in range(2)]
+        first_product(0, 3, 0)
+        first_product(1, 3, 0)
+        for c in range(J_CHUNKS):
+            scores(2, c, [2, 3, 4][c])
+        add_bias(0, 3)
+        for c in range(J_CHUNKS):
+            chunk_maximum(2, c)
+        quantise_q(0, 3, 1)
+        row_maximum(2)
+        for i in range(2):
+            weighted_total(i)
+        whole_row(2)
+
+        first_product(2, 3, 1)
+        first_product(3, 3, 1)
+        for c in range(J_CHUNKS):
+            open_scores(3, c, [6, 7, 5][c])
+            score_pass(3, c, 0)
+        add_bias(1, 3)
+        invert(0)
+        quantise_q(1, 3, 1)
+        invert(1)
+        for i in range(2):
+            nc.vector.tensor_scalar_mul(factor[i][:], weights[i][:], inverse[i][:])
+        for i in range(2):
+            finish_by_scalar(i)
+
+        for c in range(J_CHUNKS):
+            score_pass(3, c, 1)
+        for c in range(J_CHUNKS):
+            chunk_maximum(3, c)
+        total(2)
+        row_maximum(3)
+        invert(2)
+        for i in range(3):
+            finish_by_vector(i)
+        whole_row(3)
+        total(3)
+        invert(3)
+        finish_by_vector(3)

@@ -209,8 +209,14 @@ def tile_visualdeconfounder_pa_kernel(tc, x, Wy_w, Wy_b, k, prior, out):
         row_max = [small.tile([P, 1], F32, name="row_max%d" % i) for i in range(N_BLOCKS)]
         row_shift = [small.tile([P, 1], F32, name="row_shift%d" % i) for i in range(N_BLOCKS)]
         shift = [small.tile([P, J_CHUNKS], F32, name="shift%d" % i) for i in range(N_BLOCKS)]
-        chunk_sum = [small.tile([P, J_CHUNKS], F32, name="chunk_sum%d" % i) for i in range(N_BLOCKS)]
-        factor = [small.tile([P, J_CHUNKS], F32, name="factor%d" % i) for i in range(N_BLOCKS)]
+        pair_sum = small.tile([P, 2, J_CHUNKS], F32)
+        pair_weight = small.tile([P, 2, J_CHUNKS], F32)
+        pair_factor = small.tile([P, 2, J_CHUNKS], F32)
+        chunk_sum = [pair_sum[:, i] for i in range(2)]
+        for i in range(2, N_BLOCKS):
+            sums = small.tile([P, J_CHUNKS], F32, name="chunk_sum%d" % i)
+            chunk_sum.append(sums[:])
+        factor = [pair_factor[:, i] for i in range(2)]
 
         def columns(c):
             return slice(BANK * c, BANK * (c + 1))
@@ -275,51 +281,55 @@ def tile_visualdeconfounder_pa_kernel(tc, x, Wy_w, Wy_b, k, prior, out):
                 exponential(i, c, row_shift[i][:])
 
         def chunk_weights(i):
-            weight = small.tile([P, J_CHUNKS], F32)
             negated(row_shift[i][:], row_max[i][:])
             nc.scalar.activation(
-                out=weight[:], in_=chunk_max[i][:], func=ACT.Exp, bias=row_shift[i][:], scale=SCALE
+                out=pair_weight[:, i], in_=chunk_max[i][:], func=ACT.Exp, bias=row_shift[i][:], scale=SCALE
             )
-            return weight
 
         row_sum = [small.tile([P, 1], F32, name="row_sum%d" % i) for i in range(N_BLOCKS)]
         inverse = [small.tile([P, 1], F32, name="inverse%d" % i) for i in range(N_BLOCKS)]
 
-        def weighted_total(i):
-            weighted = small.tile([P, J_CHUNKS], F32)
-            nc.vector.scalar_tensor_tensor(
-                out=weighted[:], in0=weights[i][:], scalar=1.0, in1=chunk_sum[i][:],
-                op0=ALU.mult, op1=ALU.mult, accum_out=row_sum[i][:],
+        pair_inverse = small.tile([P, 2], F32)
+        pair_total = small.tile([P, 2], F32)
+
+        def pair_totals():
+            weighted = small.tile([P, 2, J_CHUNKS], F32)
+            two = small.tile([P, 2], F32)
+            nc.gpsimd.tensor_tensor(out=weighted[:], in0=pair_weight[:], in1=pair_sum[:], op=ALU.mult)
+            nc.gpsimd.tensor_tensor(out=two[:], in0=weighted[:, :, 0], in1=weighted[:, :, 1], op=ALU.add)
+            nc.gpsimd.tensor_tensor(out=pair_total[:], in0=two[:], in1=weighted[:, :, 2], op=ALU.add)
+
+        def pair_factors():
+            nc.gpsimd.tensor_tensor(
+                out=pair_factor[:],
+                in0=pair_weight[:],
+                in1=pair_inverse[:].unsqueeze(2).to_broadcast([P, 2, J_CHUNKS]),
+                op=ALU.mult,
             )
 
         def total(i):
-            nc.vector.tensor_reduce(out=row_sum[i][:], in_=chunk_sum[i][:], axis=AXIS.X, op=ALU.add)
+            nc.vector.tensor_reduce(out=row_sum[i][:], in_=chunk_sum[i], axis=AXIS.X, op=ALU.add)
 
         def invert(i):
             nc.vector.reciprocal(inverse[i][:], row_sum[i][:])
 
-        def store(i, c):
-            nc.sync.dma_start(out=out[P * i : P * (i + 1), columns(c)], in_=result[i][:, columns(c)])
+        def scale(i, c):
+            part = result[i][:, columns(c)]
+            nc.scalar.activation(out=part, in_=part, func=ACT.Copy, scale=factor[i][:, c : c + 1])
 
-        def finish_by_scalar(i):
-            for c in range(J_CHUNKS):
-                if by_gpsimd(i, c):
-                    part = result[i][:, columns(c)]
-                    nc.scalar.activation(out=part, in_=part, func=ACT.Copy, scale=factor[i][:, c : c + 1])
-                    store(i, c)
+        def weigh(i, c):
+            nc.vector.scalar_tensor_tensor(
+                out=result[i][:, columns(c)],
+                in0=soft_e[i][:, columns(c)],
+                scalar=factor[i][:, c : c + 1] if i < 2 else inverse[i][:],
+                in1=prior_all[:, columns(c)],
+                op0=ALU.mult,
+                op1=ALU.mult,
+            )
 
-        def finish_by_vector(i):
-            for c in range(J_CHUNKS):
-                if not by_gpsimd(i, c):
-                    nc.vector.scalar_tensor_tensor(
-                        out=result[i][:, columns(c)],
-                        in0=soft_e[i][:, columns(c)],
-                        scalar=factor[i][:, c : c + 1] if i < 2 else inverse[i][:],
-                        in1=prior_all[:, columns(c)],
-                        op0=ALU.mult,
-                        op1=ALU.mult,
-                    )
-                    store(i, c)
+        def store(i, first, last):
+            cols = slice(BANK * first, BANK * (last + 1))
+            nc.sync.dma_start(out=out[P * i : P * (i + 1), cols], in_=result[i][:, cols])
 
         units = x_units[:2] + w_units + k_units[:2] + [x_units[2], k_units[2], x_units[3]]
         unit_banks = [
@@ -376,7 +386,9 @@ def tile_visualdeconfounder_pa_kernel(tc, x, Wy_w, Wy_b, k, prior, out):
         for i in range(2):
             row_maximum(i)
         exponentials(chunks[10])
-        weights = [chunk_weights(i) for i in range(2)]
+        for i in range(2):
+            chunk_weights(i)
+        pair_totals()
         first_product(0, 3, 0)
         first_product(1, 3, 0)
         for c in range(J_CHUNKS):
@@ -386,24 +398,24 @@ def tile_visualdeconfounder_pa_kernel(tc, x, Wy_w, Wy_b, k, prior, out):
             chunk_maximum(2, c)
         quantise_q(0, 3, 1)
         row_maximum(2)
-        for i in range(2):
-            weighted_total(i)
+        nc.vector.reciprocal(pair_inverse[:], pair_total[:])
+        pair_factors()
         whole_row(2)
-
         first_product(2, 3, 1)
         first_product(3, 3, 1)
         for c in range(J_CHUNKS):
             open_scores(3, c, [6, 7, 5][c])
             score_pass(3, c, 0)
         add_bias(1, 3)
-        invert(0)
         quantise_q(1, 3, 1)
-        invert(1)
-        for i in range(2):
-            nc.vector.tensor_scalar_mul(factor[i][:], weights[i][:], inverse[i][:])
-        for i in range(2):
-            finish_by_scalar(i)
-
+        weigh(0, 2)
+        store(0, 2, 2)
+        scale(0, 0)
+        scale(0, 1)
+        store(0, 0, 1)
+        scale(1, 0)
+        scale(1, 1)
+        store(1, 0, 1)
         for c in range(J_CHUNKS):
             score_pass(3, c, 1)
         for c in range(J_CHUNKS):
@@ -411,9 +423,19 @@ def tile_visualdeconfounder_pa_kernel(tc, x, Wy_w, Wy_b, k, prior, out):
         total(2)
         row_maximum(3)
         invert(2)
-        for i in range(3):
-            finish_by_vector(i)
+        weigh(1, 2)
+        store(1, 2, 2)
+        weigh(2, 0)
+        weigh(2, 1)
+        store(2, 0, 1)
+        weigh(2, 2)
+        store(2, 2, 2)
         whole_row(3)
         total(3)
         invert(3)
-        finish_by_vector(3)
+        weigh(3, 0)
+        store(3, 0, 0)
+        weigh(3, 1)
+        store(3, 1, 1)
+        weigh(3, 2)
+        store(3, 2, 2)

@@ -66,9 +66,9 @@ def tile_visualdeconfounder_pa_kernel(tc, x, Wy_w, Wy_b, k, prior, out):
             nc.sync.dma_start(out=x_raw[i][:], in_=x[P * i : P * (i + 1), :])
 
         load_x(0)
-        load_x(1)
         load_w(0)
         load_w(1)
+        load_x(1)
         bias = const.tile([P, 8], BF16)
         with nc.allow_non_contiguous_dma(reason="1,024 bias values, four to a piece"):
             nc.sync.dma_start(
@@ -159,7 +159,7 @@ def tile_visualdeconfounder_pa_kernel(tc, x, Wy_w, Wy_b, k, prior, out):
             for c in range(4)
         ]
         k_units = [
-            (k_raw[c], 4, True, c < 2, k_codes, k_scales, [BANK * c, K_DICT + BANK * c])
+            (k_raw[c], 4, True, c < 2, k_codes, k_scales, [2 * BANK * c, 2 * BANK * c + BANK])
             for c in range(J_CHUNKS)
         ]
 
@@ -228,7 +228,7 @@ def tile_visualdeconfounder_pa_kernel(tc, x, Wy_w, Wy_b, k, prior, out):
             mx_pass(
                 s_banks[i, c][:].rearrange("p t n -> p (t n)"),
                 q_codes, q_scales, g * N_ROWS + P * i,
-                k_codes, k_scales, g * K_DICT + BANK * c,
+                k_codes, k_scales, (E_PASSES * c + g) * BANK,
                 BANK, g, E_PASSES,
             )
 
@@ -331,22 +331,23 @@ def tile_visualdeconfounder_pa_kernel(tc, x, Wy_w, Wy_b, k, prior, out):
             cols = slice(BANK * first, BANK * (last + 1))
             nc.sync.dma_start(out=out[P * i : P * (i + 1), cols], in_=result[i][:, cols])
 
-        units = x_units[:2] + w_units + k_units[:2] + [x_units[2], k_units[2], x_units[3]]
+        units = x_units[:1] + w_units[:2] + x_units[1:2] + w_units[2:] + k_units[:2] + [x_units[2], k_units[2], x_units[3]]
         unit_banks = [
-            [0, 1], [2, 3], [4, 5, 6, 7], [0, 1, 2, 3], [6, 7, 0, 1], [2, 3, 6, 7],
-            [4, 5, 2, 3], [6, 7, 4, 5], [2, 3], [0, 1, 4, 5], [0, 1],
+            [0, 1], [4, 5, 6, 7], [0, 1, 2, 3], [6, 7], [0, 1, 2, 3], [6, 7, 0, 1],
+            [4, 5, 6, 7], [0, 1, 4, 5], [6, 7], [0, 1, 4, 5], [0, 1],
         ]
         products = {
-            3: [(0, 0, 4), (0, 1, 5)],
-            4: [(1, 0, 4), (1, 1, 5)],
-            5: [(2, 0, 0), (2, 1, 1)],
-            6: [(3, 0, 0), (3, 1, 1)],
+            2: [(0, 0, 4)],
+            3: [(1, 0, 4)],
+            4: [(0, 1, 5), (1, 1, 5)],
+            5: [(2, 0, 2), (2, 1, 3)],
+            6: [(3, 0, 2), (3, 1, 3)],
             10: [(0, 2, 4), (1, 2, 4), (2, 2, 5), (3, 2, 5)],
         }
         chunks = {
-            8: [(0, 0, 6), (1, 0, 7)],
-            9: [(0, 1, 2), (1, 1, 3)],
-            10: [(0, 2, 6), (1, 2, 7)],
+            8: [(0, 0, 2), (1, 0, 3)],
+            9: [(0, 1, 6), (1, 1, 7)],
+            10: [(0, 2, 2), (1, 2, 3)],
         }
 
         def finished_q(j):
@@ -365,7 +366,10 @@ def tile_visualdeconfounder_pa_kernel(tc, x, Wy_w, Wy_b, k, prior, out):
             if following:
                 for h in range(2):
                     split_half(following, next_words, h)
-            quantising = [partial(quantise_half, unit, grouped, h) for h in range(2)]
+            if unit[2]:
+                quantising = [partial(quantise, grouped[:], k_codes, k_scales, unit[6][0], 2 * BANK)]
+            else:
+                quantising = [partial(quantise_half, unit, grouped, h) for h in range(2)]
             biasing = [partial(add_bias, g, i) for g, i in finished_q(j)]
             if unit[2]:
                 work = biasing[:1] + quantising + biasing[1:]
@@ -392,7 +396,7 @@ def tile_visualdeconfounder_pa_kernel(tc, x, Wy_w, Wy_b, k, prior, out):
         first_product(0, 3, 0)
         first_product(1, 3, 0)
         for c in range(J_CHUNKS):
-            scores(2, c, [2, 3, 4][c])
+            scores(2, c, [6, 7, 4][c])
         add_bias(0, 3)
         for c in range(J_CHUNKS):
             chunk_maximum(2, c)
@@ -404,7 +408,7 @@ def tile_visualdeconfounder_pa_kernel(tc, x, Wy_w, Wy_b, k, prior, out):
         first_product(2, 3, 1)
         first_product(3, 3, 1)
         for c in range(J_CHUNKS):
-            open_scores(3, c, [6, 7, 5][c])
+            open_scores(3, c, [2, 3, 5][c])
             score_pass(3, c, 0)
         add_bias(1, 3)
         quantise_q(1, 3, 1)

@@ -69,12 +69,6 @@ def tile_visualdeconfounder_pa_kernel(tc, x, Wy_w, Wy_b, k, prior, out):
         load_w(0)
         load_w(1)
         load_x(1)
-        bias = const.tile([P, 8], BF16)
-        with nc.allow_non_contiguous_dma(reason="1,024 bias values, four to a piece"):
-            nc.sync.dma_start(
-                out=bias[:].rearrange("p (g t) -> p g t", t=4),
-                in_=Wy_b.rearrange("(g p t) -> p g t", p=P, t=4),
-            )
         load_w(2)
         load_w(3)
         load_k(0)
@@ -89,6 +83,13 @@ def tile_visualdeconfounder_pa_kernel(tc, x, Wy_w, Wy_b, k, prior, out):
         one = const.tile([P, 1], F32)
         nc.vector.memset(zero[:], 0.0)
         nc.scalar.activation(out=one[:], in_=zero[:], func=ACT.Exp)
+
+        bias = const.tile([P, 8], BF16)
+        with nc.allow_non_contiguous_dma(reason="1,024 bias values, four to a piece"):
+            nc.scalar.dma_start(
+                out=bias[:].rearrange("p (g t) -> p g t", t=4),
+                in_=Wy_b.rearrange("(g p t) -> p g t", p=P, t=4),
+            )
 
         ident = const.tile([P, P], F32)
         masks.make_identity(nc, ident[:])
@@ -153,7 +154,7 @@ def tile_visualdeconfounder_pa_kernel(tc, x, Wy_w, Wy_b, k, prior, out):
                 q_codes, q_scales, g * N_ROWS + P * i, P * blocks,
             )
 
-        x_units = [(x_raw[i], 2, False, False, x_codes, x_scales, [i * BANK]) for i in range(N_BLOCKS)]
+        x_units = [(x_raw[i], 2, False, i in (1, 3), x_codes, x_scales, [i * BANK]) for i in range(N_BLOCKS)]
         w_units = [
             (w_raw[c], 4, False, c > 1, w_codes, w_scales, [2 * c * BANK, (2 * c + 1) * BANK])
             for c in range(4)
@@ -402,8 +403,6 @@ def tile_visualdeconfounder_pa_kernel(tc, x, Wy_w, Wy_b, k, prior, out):
             chunk_maximum(2, c)
         quantise_q(0, 3, 1)
         row_maximum(2)
-        nc.vector.reciprocal(pair_inverse[:], pair_total[:])
-        pair_factors()
         whole_row(2)
         first_product(2, 3, 1)
         first_product(3, 3, 1)
@@ -411,6 +410,8 @@ def tile_visualdeconfounder_pa_kernel(tc, x, Wy_w, Wy_b, k, prior, out):
             open_scores(3, c, [2, 3, 5][c])
             score_pass(3, c, 0)
         add_bias(1, 3)
+        nc.vector.reciprocal(pair_inverse[:], pair_total[:])
+        pair_factors()
         quantise_q(1, 3, 1)
         weigh(0, 2)
         store(0, 2, 2)

from contextlib import ExitStack
from functools import partial

import concourse.masks as masks
import concourse.mybir as mybir

F32 = mybir.dt.float32
BF16 = mybir.dt.bfloat16
U32 = mybir.dt.uint32
U8 = mybir.dt.uint8
FP8X4 = mybir.dt.float8_e4m3fn_x4
ALU = mybir.AluOpType
ACT = mybir.ActivationFunctionType
AXIS = mybir.AxisListType

P = 128
BANK = 512
N_ROWS, F_DIM, E_DIM, K_DICT = 512, 2048, 1024, 1536
N_BLOCKS = N_ROWS // P
F_PASSES = F_DIM // 512
E_PASSES = E_DIM // 512
J_CHUNKS = K_DICT // BANK
UNIT = 4096
SCALE = 1.0 / (E_DIM**0.5)

FLOPS = 2 * N_ROWS * F_DIM * E_DIM + 2 * N_ROWS * E_DIM * K_DICT


def tile_visualdeconfounder_pa_kernel(tc, x, Wy_w, Wy_b, k, prior, out):
    nc = tc.nc
    with ExitStack() as ctx:
        ctx.enter_context(tc.manual_schedule())
        const = ctx.enter_context(tc.tile_pool(name="const", bufs=1))
        raw_pool = ctx.enter_context(tc.tile_pool(name="raw", bufs=1))
        keep = ctx.enter_context(tc.tile_pool(name="keep", bufs=1))
        split_pool = ctx.enter_context(tc.tile_pool(name="split", bufs=2))
        grouped_pool = ctx.enter_context(tc.tile_pool(name="grouped", bufs=3))
        soft = ctx.enter_context(tc.tile_pool(name="soft", bufs=1))
        small = ctx.enter_context(tc.tile_pool(name="small", bufs=4))
        psum = ctx.enter_context(tc.psum_pool(name="psum", bufs=1))

        def new_bank(b):
            return psum.tile([P, 4, P], F32, name="bank%d" % b)

        x_raw = [raw_pool.tile([P, F_DIM], BF16, name="x_raw%d" % i) for i in range(N_BLOCKS)]
        w_raw = [raw_pool.tile([P, UNIT], BF16, name="w_raw%d" % c) for c in range(4)]
        k_raw = [raw_pool.tile([P, UNIT], BF16, name="k_raw%d" % c) for c in range(J_CHUNKS)]

        def load_w(c):
            g, h = divmod(c, 2)
            rows = Wy_w[512 * g : 512 * (g + 1), :].rearrange("(p t) f -> p t f", t=4)
            for s in range(2):
                nc.sync.dma_start(
                    out=w_raw[c][:, F_DIM * s : F_DIM * (s + 1)], in_=rows[:, 2 * h + s, :]
                )

        def load_k(c):
            for half in range(2):
                first = BANK * c + 2 * P * half
                nc.sync.dma_start(
                    out=k_raw[c][:, 2048 * half : 2048 * (half + 1)].rearrange("p (b e) -> p b e", b=2),
                    in_=k[first : first + 2 * P, :].rearrange("(b p) e -> p b e", p=P),
                )

        def load_x(i):
            nc.sync.dma_start(out=x_raw[i][:], in_=x[P * i : P * (i + 1), :])

        load_x(0)
        load_w(0)
        load_w(1)
        load_x(1)
        load_w(2)
        load_w(3)
        load_k(0)
        load_k(1)
        load_x(2)
        load_k(2)
        load_x(3)
        prior_all = const.tile([P, K_DICT], BF16)
        nc.sync.dma_start(out=prior_all[:], in_=prior.partition_broadcast(P))

        zero = const.tile([P, 1], F32)
        one = const.tile([P, 1], F32)
        nc.vector.memset(zero[:], 0.0)
        nc.scalar.activation(out=one[:], in_=zero[:], func=ACT.Exp)

        bias = const.tile([P, 8], BF16)
        with nc.allow_non_contiguous_dma(reason="1,024 bias values, four to a piece"):
            nc.scalar.dma_start(
                out=bias[:].rearrange("p (g t) -> p g t", t=4),
                in_=Wy_b.rearrange("(g p t) -> p g t", p=P, t=4),
            )

        ident = const.tile([P, P], F32)
        masks.make_identity(nc, ident[:])

        x_codes = keep.tile([P, N_BLOCKS * F_PASSES * P], U32, align_bytes=64)
        x_scales = keep.tile([P, N_BLOCKS * F_PASSES * P], U8, align_bytes=64)
        w_codes = keep.tile([P, 8 * F_PASSES * P], U32, align_bytes=64)
        w_scales = keep.tile([P, 8 * F_PASSES * P], U8, align_bytes=64)
        k_codes = keep.tile([P, E_PASSES * K_DICT], U32, align_bytes=64)
        k_scales = keep.tile([P, E_PASSES * K_DICT], U8, align_bytes=64)
        q_codes = keep.tile([P, E_PASSES * N_ROWS], U32, align_bytes=64)
        q_scales = keep.tile([P, E_PASSES * N_ROWS], U8, align_bytes=64)
        q_grouped = [
            keep.tile([P, N_ROWS * 4], BF16, name="q_grouped%d" % g, align_bytes=64)
            for g in range(E_PASSES)
        ]

        def quantise(grouped, codes, scales, first, width):
            nc.vector.quantize_mx(
                out=codes[:, first : first + width].bitcast(FP8X4),
                scales=scales[:, first : first + width],
                in_=grouped,
            )

        def mx_pass(acc, a_codes, a_scales, a_first, b_codes, b_scales, b_first, width, g, passes):
            nc.tensor.matmul_mx(
                out=acc,
                lhsT=a_codes[:, a_first : a_first + P].bitcast(FP8X4),
                lhsT_scale=a_scales[:, a_first : a_first + P],
                rhs=b_codes[:, b_first : b_first + width].bitcast(FP8X4),
                rhs_scale=b_scales[:, b_first : b_first + width],
                start=(g == 0),
                stop=(g == passes - 1),
            )

        q_banks = {}

        def first_product(c, i, bank):
            g, h = divmod(c, 2)
            if h == 0:
                q_banks[g, i] = new_bank(bank)
            for s in range(2):
                for f in range(F_PASSES):
                    mx_pass(
                        q_banks[g, i][:, 2 * h + s, :],
                        w_codes, w_scales, ((2 * c + s) * F_PASSES + f) * P,
                        x_codes, x_scales, (i * F_PASSES + f) * P,
                        P, f, F_PASSES,
                    )

        def add_bias(g, i):
            nc.vector.tensor_tensor(
                out=q_grouped[g][:, BANK * i : BANK * (i + 1)].rearrange("p (n t) -> p n t", t=4),
                in0=q_banks[g, i][:].rearrange("p t n -> p n t"),
                in1=bias[:, 4 * g : 4 * g + 4].unsqueeze(1).to_broadcast([P, P, 4]),
                op=ALU.add,
            )

        def quantise_q(g, i, blocks):
            quantise(
                q_grouped[g][:, BANK * i : BANK * (i + blocks)],
                q_codes, q_scales, g * N_ROWS + P * i, P * blocks,
            )

        x_units = [(x_raw[i], 2, False, i in (1, 3), x_codes, x_scales, [i * BANK]) for i in range(N_BLOCKS)]
        w_units = [
            (w_raw[c], 4, False, c > 1, w_codes, w_scales, [2 * c * BANK, (2 * c + 1) * BANK])
            for c in range(4)
        ]
        k_units = [
            (k_raw[c], 4, True, c < 2, k_codes, k_scales, [2 * BANK * c, 2 * BANK * c + BANK])
            for c in range(J_CHUNKS)
        ]

        def new_words(unit):
            if not unit[3]:
                return unit[0][:].bitcast(F32)
            split = split_pool.tile([P, UNIT // 2], F32, name="split")
            return split[:]

        def split_half(unit, words, h):
            if unit[3] and h < len(unit[6]):
                cols = slice(1024 * h, 1024 * (h + 1))
                nc.vector.tensor_copy(
                    out=words[:, cols].rearrange("p (g u m) -> p g u m", u=2, m=P),
                    in_=unit[0][:].bitcast(F32)[:, cols].rearrange("p (g m u) -> p g u m", u=2, m=P),
                )

        def transpose_unit(unit, words, banks, vector_banks=()):
            grouped = grouped_pool.tile([P, UNIT], BF16, align_bytes=64)
            order = "p (g b r u) -> p b g r u" if unit[2] else "p (b g r u) -> p b g r u"
            dest = grouped[:, : 1024 * unit[1]].bitcast(F32).rearrange(order, g=2, b=unit[1], u=2)
            for b in range(unit[1]):
                bank = new_bank(banks[b])
                for v in range(4):
                    g, u = divmod(v, 2)
                    first = BANK * b + 2 * P * g
                    if unit[3]:
                        plane = words[:, first + P * u : first + P * (u + 1)]
                    else:
                        plane = words[:, first + u : first + 2 * P : 2]
                    nc.tensor.transpose(bank[:, v, :], plane, ident[:])
                source = bank[:].rearrange("p (g u) r -> p g r u", u=2)
                if b in vector_banks:
                    nc.vector.tensor_copy(out=dest[:, b], in_=source)
                else:
                    nc.scalar.copy(out=dest[:, b], in_=source)
            return grouped

        def quantise_half(unit, grouped, h):
            if h < len(unit[6]):
                quantise(grouped[:, 2048 * h : 2048 * (h + 1)], unit[4], unit[5], unit[6][h], BANK)

        s_banks = {}
        soft_e = [soft.tile([P, K_DICT], F32, name="soft_e%d" % i) for i in range(N_BLOCKS)]
        result = [soft.tile([P, K_DICT], F32, name="result%d" % i) for i in range(N_BLOCKS)]
        chunk_max = [small.tile([P, J_CHUNKS], F32, name="chunk_max%d" % i) for i in range(N_BLOCKS)]
        row_max = [small.tile([P, 1], F32, name="row_max%d" % i) for i in range(N_BLOCKS)]
        row_shift = [small.tile([P, 1], F32, name="row_shift%d" % i) for i in range(N_BLOCKS)]
        shift = [small.tile([P, J_CHUNKS], F32, name="shift%d" % i) for i in range(N_BLOCKS)]
        pair_sum = small.tile([P, 2, J_CHUNKS], F32)
        pair_weight = small.tile([P, 2, J_CHUNKS], F32)
        pair_factor = small.tile([P, 2, J_CHUNKS], F32)
        chunk_sum = [pair_sum[:, i] for i in range(2)]
        for i in range(2, N_BLOCKS):
            sums = small.tile([P, J_CHUNKS], F32, name="chunk_sum%d" % i)
            chunk_sum.append(sums[:])
        factor = [pair_factor[:, i] for i in range(2)]

        def columns(c):
            return slice(BANK * c, BANK * (c + 1))

        def open_scores(i, c, bank):
            s_banks[i, c] = new_bank(bank)

        def score_pass(i, c, g):
            mx_pass(
                s_banks[i, c][:].rearrange("p t n -> p (t n)"),
                q_codes, q_scales, g * N_ROWS + P * i,
                k_codes, k_scales, (E_PASSES * c + g) * BANK,
                BANK, g, E_PASSES,
            )

        def scores(i, c, bank):
            open_scores(i, c, bank)
            for g in range(E_PASSES):
                score_pass(i, c, g)

        def chunk_maximum(i, c):
            nc.vector.tensor_reduce(
                out=chunk_max[i][:, c : c + 1],
                in_=s_banks[i, c][:].rearrange("p t n -> p (t n)"), axis=AXIS.X, op=ALU.max,
            )

        def by_gpsimd(i, c):
            return i < 2 and c < J_CHUNKS - 1

        def row_maximum(i):
            nc.vector.tensor_reduce(out=row_max[i][:], in_=chunk_max[i][:], axis=AXIS.X, op=ALU.max)

        def negated(out, maxima):
            nc.scalar.activation(out=out, in_=maxima, func=ACT.Copy, scale=-SCALE)

        def exponential(i, c, bias):
            nc.scalar.activation(
                out=soft_e[i][:, columns(c)],
                in_=s_banks[i, c][:].rearrange("p t n -> p (t n)"),
                func=ACT.Exp,
                bias=bias,
                scale=SCALE,
                accum_out=chunk_sum[i][:, c : c + 1],
            )
            if by_gpsimd(i, c):
                nc.gpsimd.tensor_tensor(
                    out=result[i][:, columns(c)],
                    in0=soft_e[i][:, columns(c)],
                    in1=prior_all[:, columns(c)],
                    op=ALU.mult,
                )

        def exponentials(scored):
            for i, c, bank in scored:
                negated(shift[i][:, c : c + 1], chunk_max[i][:, c : c + 1])
            for i, c, bank in scored:
                exponential(i, c, shift[i][:, c : c + 1])

        def whole_row(i):
            negated(row_shift[i][:], row_max[i][:])
            for c in range(J_CHUNKS):
                exponential(i, c, row_shift[i][:])

        def chunk_weights(i):
            negated(row_shift[i][:], row_max[i][:])
            nc.scalar.activation(
                out=pair_weight[:, i], in_=chunk_max[i][:], func=ACT.Exp, bias=row_shift[i][:], scale=SCALE
            )

        row_sum = [small.tile([P, 1], F32, name="row_sum%d" % i) for i in range(N_BLOCKS)]
        inverse = [small.tile([P, 1], F32, name="inverse%d" % i) for i in range(N_BLOCKS)]

        pair_inverse = small.tile([P, 2], F32)
        pair_total = small.tile([P, 2], F32)

        def pair_totals():
            weighted = small.tile([P, 2, J_CHUNKS], F32)
            two = small.tile([P, 2], F32)
            nc.gpsimd.tensor_tensor(out=weighted[:], in0=pair_weight[:], in1=pair_sum[:], op=ALU.mult)
            nc.gpsimd.tensor_tensor(out=two[:], in0=weighted[:, :, 0], in1=weighted[:, :, 1], op=ALU.add)
            nc.gpsimd.tensor_tensor(out=pair_total[:], in0=two[:], in1=weighted[:, :, 2], op=ALU.add)

        def pair_factors():
            nc.gpsimd.tensor_tensor(
                out=pair_factor[:],
                in0=pair_weight[:],
                in1=pair_inverse[:].unsqueeze(2).to_broadcast([P, 2, J_CHUNKS]),
                op=ALU.mult,
            )

        def total(i):
            nc.vector.tensor_reduce(out=row_sum[i][:], in_=chunk_sum[i], axis=AXIS.X, op=ALU.add)

        def invert(i):
            nc.vector.reciprocal(inverse[i][:], row_sum[i][:])

        def scale(i, c):
            part = result[i][:, columns(c)]
            nc.scalar.activation(out=part, in_=part, func=ACT.Copy, scale=factor[i][:, c : c + 1])

        def weigh(i, c):
            nc.vector.scalar_tensor_tensor(
                out=result[i][:, columns(c)],
                in0=soft_e[i][:, columns(c)],
                scalar=factor[i][:, c : c + 1] if i < 2 else inverse[i][:],
                in1=prior_all[:, columns(c)],
                op0=ALU.mult,
                op1=ALU.mult,
            )

        def store(i, first, last):
            cols = slice(BANK * first, BANK * (last + 1))
            nc.sync.dma_start(out=out[P * i : P * (i + 1), cols], in_=result[i][:, cols])

        units = x_units[:1] + w_units[:2] + x_units[1:2] + w_units[2:] + k_units[:2] + [x_units[2], k_units[2], x_units[3]]
        unit_banks = [
            [0, 1], [4, 5, 6, 7], [0, 1, 2, 3], [6, 7], [0, 1, 2, 3], [6, 7, 0, 1],
            [4, 5, 6, 7], [0, 1, 4, 5], [6, 7], [0, 1, 4, 5], [0, 1],
        ]
        products = {
            2: [(0, 0, 4)],
            3: [(1, 0, 4)],
            4: [(0, 1, 5), (1, 1, 5)],
            5: [(2, 0, 2), (2, 1, 3)],
            6: [(3, 0, 2), (3, 1, 3)],
            10: [(0, 2, 4), (1, 2, 4), (2, 2, 5), (3, 2, 5)],
        }
        chunks = {
            8: [(0, 0, 2), (1, 0, 3)],
            9: [(0, 1, 6), (1, 1, 7)],
            10: [(0, 2, 2), (1, 2, 3)],
        }

        def finished_q(j):
            return [(c // 2, i) for c, i, bank in products.get(j, []) if c % 2 == 1]

        def step(j, words):
            unit = units[j]
            following = units[j + 1] if j + 1 < len(units) else None
            next_words = new_words(following) if following else None
            grouped = transpose_unit(unit, words, unit_banks[j], (1,) if j < 2 else ())
            exponentials(chunks.get(j - 1, []))
            for product in products.get(j, []):
                first_product(*product)
            for i, c, bank in chunks.get(j, []):
                scores(i, c, bank)
            if following:
                for h in range(2):
                    split_half(following, next_words, h)
            if unit[2]:
                quantising = [partial(quantise, grouped[:], k_codes, k_scales, unit[6][0], 2 * BANK)]
            else:
                quantising = [partial(quantise_half, unit, grouped, h) for h in range(2)]
            biasing = [partial(add_bias, g, i) for g, i in finished_q(j)]
            if unit[2]:
                work = biasing[:1] + quantising + biasing[1:]
            else:
                work = quantising[:1] + biasing[:1] + quantising[1:] + biasing[1:]
            for task in work:
                task()
            for i, c, bank in chunks.get(j, []):
                chunk_maximum(i, c)
            for g, i in finished_q(j):
                quantise_q(g, i, 1)
            return next_words

        words = new_words(units[0])
        for j in range(len(units)):
            words = step(j, words)

        for i in range(2):
            row_maximum(i)
        exponentials(chunks[10])
        for i in range(2):
            chunk_weights(i)
        pair_totals()
        first_product(0, 3, 0)
        first_product(1, 3, 0)
        for c in range(J_CHUNKS):
            scores(2, c, [6, 7, 4][c])
        add_bias(0, 3)
        for c in range(J_CHUNKS):
            chunk_maximum(2, c)
        quantise_q(0, 3, 1)
        row_maximum(2)
        whole_row(2)
        first_product(2, 3, 1)
        first_product(3, 3, 1)
        for c in range(J_CHUNKS):
            open_scores(3, c, [2, 3, 5][c])
            score_pass(3, c, 0)
        add_bias(1, 3)
        nc.vector.reciprocal(pair_inverse[:], pair_total[:])
        pair_factors()
        quantise_q(1, 3, 1)
        weigh(0, 2)
        store(0, 2, 2)
        scale(0, 0)
        scale(0, 1)
        store(0, 0, 1)
        scale(1, 0)
        scale(1, 1)
        store(1, 0, 1)
        for c in range(J_CHUNKS):
            score_pass(3, c, 1)
        for c in range(J_CHUNKS):
            chunk_maximum(3, c)
        total(2)
        row_maximum(3)
        invert(2)
        weigh(1, 2)
        store(1, 2, 2)
        weigh(2, 0)
        weigh(2, 1)
        store(2, 0, 1)
        weigh(2, 2)
        store(2, 2, 2)
        whole_row(3)
        total(3)
        invert(3)
        weigh(3, 0)
        store(3, 0, 0)
        weigh(3, 1)
        store(3, 1, 1)
        weigh(3, 2)
        store(3, 2, 2)
